import numpy as np
import ml_dtypes


def mxq(x, axis, fmt="e4m3"):
    dtype, down = {"e4m3": (ml_dtypes.float8_e4m3fn, 7), "e5m2": (ml_dtypes.float8_e5m2, 14)}[fmt]
    v = np.moveaxis(np.asarray(x, np.float32).astype(ml_dtypes.bfloat16).astype(np.float64), axis, -1)
    blocks = v.reshape(v.shape[:-1] + (-1, 32))
    amax = np.abs(blocks).max(-1, keepdims=True)
    byte = np.maximum(np.where(amax > 0, np.frexp(amax)[1] - 1 + 127, 0) - down, 1)
    scale = np.exp2(byte - 127.0)
    codes = (blocks / scale).astype(np.float32).astype(dtype).astype(np.float64)
    return np.moveaxis((codes * scale).reshape(v.shape), -1, axis)


WIDE = False


def mx_kscale(k):
    if not WIDE:
        return np.ones(k)
    levels = np.array([10, -10, 5, -5, 0])
    a = np.random.permutation(np.resize(levels, k // 512 * 4)).reshape(k // 512, 4)
    idx = np.arange(k)
    return np.exp2(a[idx // 512, idx % 128 // 32])


BF16 = ml_dtypes.bfloat16


def bf(x):
    return np.asarray(x, np.float32).astype(BF16)


def f64(x):
    return np.asarray(x).astype(np.float64)


E2M1 = np.array([0.0, 0.5, 1.0, 1.5, 2.0, 3.0, 4.0, 6.0, -0.0, -0.5, -1.0, -1.5, -2.0, -3.0, -4.0, -6.0])


def pack_weight(w, fmt):
    k, n = w.shape
    w = f64(bf(w)).reshape(k // 32, 32, n)
    amax = np.abs(w).max(1)
    if fmt == "e4m3":
        byte = np.frexp(amax)[1] - 1 + 127 - 7
    else:
        mant, ex = np.frexp(amax / 6.0)
        byte = np.where(mant > 0.5, ex, ex - 1) + 127
    byte = np.clip(np.where(amax > 0, byte, 1), 1, 254)
    scaled = (w * np.exp2(127.0 - byte)[:, None, :]).reshape(k, n).astype(np.float32)
    by_word = np.ascontiguousarray(scaled.reshape(k // 512, 128, 4, n).transpose(0, 1, 3, 2))
    if fmt == "e4m3":
        words = by_word.astype(ml_dtypes.float8_e4m3fn).view(np.uint8)
    else:
        c = by_word.astype(ml_dtypes.float4_e2m1fn).view(np.uint8) & 0xF
        words = c[..., 0::2] | (c[..., 1::2] << 4)
    return np.ascontiguousarray(words), np.ascontiguousarray(byte.astype(np.uint8).reshape(k // 512, 16, n))


def unpack_weight(words, scales, fmt):
    g, p, n, _ = words.shape
    if fmt == "e4m3":
        vals = np.ascontiguousarray(words).view(ml_dtypes.float8_e4m3fn).astype(np.float64)
    else:
        nib = np.empty((g, p, n, 4), np.uint8)
        nib[..., 0::2] = words & 0xF
        nib[..., 1::2] = words >> 4
        vals = E2M1[nib]
    vals = vals * np.repeat(np.exp2(scales.astype(np.float64) - 127.0), 8, axis=1)[..., None]
    return vals.transpose(0, 1, 3, 2).reshape(g * 512, n)

def pack4(w):
    words, scales = pack_weight(w, "e2m1")
    return words.reshape(words.shape[0], 128, -1), scales


def unpack4(words, scales):
    return unpack_weight(words.reshape(words.shape[0], 128, -1, 2), scales, "e2m1")


N, MI0, MI1, MS, MG, MO0, MO1, DV = 128, 512, 256, 1024, 512, 512, 256, 3
EPS = 1e-5


def irlin_mx(x, mul0, mul1, w0, w1):
    n = x.shape[0]
    x0 = x[:, :mul0]
    x1 = x[:, mul0:].reshape(n, mul1, DV).transpose(0, 2, 1)
    y0 = (mxq(x0, 1, "e4m3") @ w0) * (1.0 / np.sqrt(mul0))
    y1 = (mxq(x1, 2, "e4m3") @ w1).transpose(0, 2, 1) * (1.0 / np.sqrt(mul1))
    return np.concatenate([y0, y1.reshape(n, -1)], axis=-1)


def irlin_plain(x, mul0, mul1, w0, w1):
    n = x.shape[0]
    x0 = x[:, :mul0]
    x1 = x[:, mul0:].reshape(n, mul1, DV).transpose(0, 2, 1)
    y0 = (x0 @ w0) * (1.0 / np.sqrt(mul0))
    y1 = (x1 @ w1).transpose(0, 2, 1) * (1.0 / np.sqrt(mul1))
    return np.concatenate([y0, y1.reshape(n, -1)], axis=-1)


def batchnorm(x, w, b):
    n = x.shape[0]
    s = x[:, :MO0]
    v = x[:, MO0:].reshape(n, MO1, DV)
    s = s - s.mean(0)
    s_inv = 1.0 / np.sqrt((s * s).mean(0) + EPS)
    s = s * (s_inv * w[:MO0]) + b
    v_inv = 1.0 / np.sqrt((v * v).mean(-1).mean(0) + EPS)
    v = v * (v_inv * w[MO0:])[None, :, None]
    return np.concatenate([s, v.reshape(n, -1)], axis=-1)


def setup_inputs():
    s0, s1 = mx_kscale(MS), mx_kscale(MG)
    h0 = (0.1 + 0.3 * np.random.standard_normal((N, MS))) * s0
    h1 = 0.28 * np.random.standard_normal((N, MG, DV)) * s1[None, :, None]
    features = bf(np.random.standard_normal((N, MI0 + DV * MI1)))
    w0_words, w0_scales = pack4(np.random.standard_normal((MS, MO0)) / s0[:, None])
    w1_words, w1_scales = pack4(np.random.standard_normal((MG, MO1)) / s1[:, None])
    return {"h2": bf(np.concatenate([h0, h1.reshape(N, -1)], axis=-1)),
            "features": features,
            "lin3_W0_words": w0_words,
            "lin3_W0_scales": w0_scales,
            "lin3_W1_words": w1_words,
            "lin3_W1_scales": w1_scales,
            "byp_W0": bf(np.random.standard_normal((MI0, MO0))),
            "byp_W1": bf(np.random.standard_normal((MI1, MO1))),
            "bn_weight": bf(1.0 + 0.1 * np.random.standard_normal(MO0 + MO1)),
            "bn_bias": bf(0.1 * np.random.standard_normal(MO0))}


def reference(h2, features, lin3_W0_words, lin3_W0_scales, lin3_W1_words, lin3_W1_scales, byp_W0, byp_W1, bn_weight, bn_bias):
    out = irlin_mx(f64(h2), MS, MG, unpack4(lin3_W0_words, lin3_W0_scales), unpack4(lin3_W1_words, lin3_W1_scales))
    out = out + irlin_plain(f64(features), MI0, MI1, f64(byp_W0), f64(byp_W1))
    return batchnorm(out, f64(bn_weight), f64(bn_bias))

@@ -1,0 +1,305 @@
+import math
+from contextlib import ExitStack
+
+import concourse.mybir as mybir
+from concourse.masks import make_identity
+
+BF16 = mybir.dt.bfloat16
+F32 = mybir.dt.float32
+I32 = mybir.dt.int32
+U32 = mybir.dt.uint32
+U8 = mybir.dt.uint8
+FP8X4 = mybir.dt.float8_e4m3fn_x4
+FP4X4 = mybir.dt.float4_e2m1fn_x4
+ALU = mybir.AluOpType
+ACT = mybir.ActivationFunctionType
+
+P = 128
+DV = 3
+HID_S, HID_V = 1024, 512
+IN_S, IN_V = 512, 256
+OUT_S, OUT_V = 512, 256
+S_BLOCKS = OUT_S // P
+V_BLOCKS = OUT_V // P
+S_PASSES = HID_S // 512
+EPS = 1e-5
+
+FLOPS = 2 * P * (HID_S * OUT_S + DV * HID_V * OUT_V + IN_S * OUT_S + DV * IN_V * OUT_V)
+
+
+def tile_feedforward_pb_s_kernel(
+    tc,
+    h2,
+    features,
+    lin3_W0_words,
+    lin3_W0_scales,
+    lin3_W1_words,
+    lin3_W1_scales,
+    byp_W0,
+    byp_W1,
+    bn_weight,
+    bn_bias,
+    out,
+):
+    nc = tc.nc
+    with ExitStack() as ctx:
+        sb = ctx.enter_context(tc.tile_pool(name="sb", bufs=1))
+        psum = ctx.enter_context(tc.psum_pool(name="psum", bufs=8))
+
+        def load_scale_rows(planes, rows):
+            for quad in range(4):
+                nc.sync.dma_start(
+                    out=planes[32 * quad : 32 * quad + 4].bitcast(I32),
+                    in_=rows.bitcast(I32)[:, 4 * quad : 4 * quad + 4, :].rearrange("g r w -> r g w"),
+                )
+
+        w1_planes = sb.tile([P, 1, OUT_V], U8, align_bytes=64)
+        w0_planes = sb.tile([P, S_PASSES, OUT_S], U8, align_bytes=64)
+        nc.vector.memset(w1_planes[:].bitcast(I32), 0)
+        nc.vector.memset(w0_planes[:].bitcast(I32), 0)
+        prm_rows = sb.tile([P, P], BF16)
+        nc.vector.memset(prm_rows[:], 0.0)
+        warm = sb.tile([P, 1], F32)
+        nc.vector.memset(warm[:], 1.0)
+        ident = sb.tile([P, P], F32)
+        make_identity(nc, ident[:])
+
+        load_scale_rows(w1_planes, lin3_W1_scales)
+        feat_sb = sb.tile([P, IN_S + IN_V * DV], BF16)
+        nc.scalar.dma_start(out=feat_sb[:], in_=features)
+        byp0_sb = sb.tile([P, 2, 2, OUT_S], BF16)
+        nc.scalar.dma_start(out=byp0_sb[:], in_=byp_W0.rearrange("(c p e) o -> p c e o", c=2, e=2))
+        h1_sb = sb.tile([P, HID_V * DV], BF16)
+        nc.scalar.dma_start(out=h1_sb[:], in_=h2[:, HID_S:])
+        h0_sb = sb.tile([P, HID_S], BF16)
+        nc.scalar.dma_start(out=h0_sb[:], in_=h2[:, :HID_S])
+        nc.scalar.activation(out=warm[:], in_=warm[:], func=ACT.Abs_reciprocal_sqrt)
+        w1_words = sb.tile([P, 2 * OUT_V], U8, align_bytes=64)
+        nc.sync.dma_start(out=w1_words[:].bitcast(I32), in_=lin3_W1_words[0].bitcast(I32))
+        w0_words = sb.tile([P, S_PASSES, 2 * OUT_S], U8, align_bytes=64)
+        nc.sync.dma_start(
+            out=w0_words[:].bitcast(I32), in_=lin3_W0_words.bitcast(I32).rearrange("g p w -> p g w")
+        )
+        byp1_sb = sb.tile([P, 2, OUT_V], BF16)
+        nc.gpsimd.dma_start(out=byp1_sb[:], in_=byp_W1.rearrange("(q a) o -> q a o", a=2))
+        load_scale_rows(w0_planes, lin3_W0_scales)
+        n_w = S_BLOCKS + V_BLOCKS
+        nc.gpsimd.dma_start(out=prm_rows[0:n_w, :], in_=bn_weight.rearrange("(b o) -> b o", o=P))
+        nc.gpsimd.dma_start(
+            out=prm_rows[n_w : n_w + S_BLOCKS, :], in_=bn_bias.rearrange("(b o) -> b o", o=P)
+        )
+
+        feat_pairs = feat_sb[:].bitcast(F32)
+        f0T = psum.tile([P, 2, P], F32, tag="bank")
+        for c in range(2):
+            nc.tensor.transpose(f0T[:, c, :], feat_pairs[:, c * P : (c + 1) * P], ident[:])
+        f1T = psum.tile([P, DV, P], F32, tag="bank")
+        for j in range(DV):
+            nc.tensor.transpose(f1T[:, j, :], feat_pairs[:, IN_S // 2 + j :: DV], ident[:])
+        f0T_sb = sb.tile([P, 2, P, 2], BF16)
+        nc.scalar.copy(
+            out=f0T_sb[:].rearrange("p c n e -> p (c n e)"),
+            in_=f0T[:].rearrange("p c n -> p (c n)").bitcast(BF16),
+        )
+        f1T_sb = sb.tile([P, DV, P, 2], BF16)
+        nc.vector.tensor_copy(
+            out=f1T_sb[:].rearrange("p j n e -> p (j n e)"),
+            in_=f1T[:].rearrange("p j n -> p (j n)").bitcast(BF16),
+        )
+
+        byp_s = psum.tile([P, S_BLOCKS, P], F32, tag="bank")
+        for b in range(S_BLOCKS):
+            for ce in range(4):
+                c, e = divmod(ce, 2)
+                nc.tensor.matmul(
+                    byp_s[:, b, :],
+                    lhsT=byp0_sb[:, c, e, b * P : (b + 1) * P],
+                    rhs=f0T_sb[:, c, :, e],
+                    start=(ce == 0),
+                    stop=(ce == 3),
+                )
+
+        h1_sorted = sb.tile([P, DV, 2, P, 2], BF16)
+        h1_by_d = h1_sb[:].rearrange("n (p u e d) -> n d u p e", u=2, e=2, d=DV)
+        nc.vector.tensor_copy(out=h1_sorted[:, 0], in_=h1_by_d[:, 0])
+        nc.scalar.copy(out=h1_sorted[:, 2], in_=h1_by_d[:, 2])
+        nc.vector.tensor_copy(out=h1_sorted[:, 1], in_=h1_by_d[:, 1])
+        grouped1 = sb.tile([P, DV, P, 4], BF16, align_bytes=64)
+        q1_codes = sb.tile([P, DV, P], U32, align_bytes=64)
+        q1_scales = sb.tile([P, DV, P], U8, align_bytes=64)
+        for d in (0, 2, 1):
+            h1_pairs = h1_sorted[:, d].rearrange("n u p e -> n (u p e)").bitcast(F32)
+            h1T = psum.tile([P, 2, P], F32, tag="bank")
+            for u in range(2):
+                nc.tensor.transpose(h1T[:, u, :], h1_pairs[:, u * P : (u + 1) * P], ident[:])
+            if d == 0:
+                nc.vector.tensor_copy(
+                    out=grouped1[:, d].bitcast(F32), in_=h1T[:].rearrange("p u n -> p n u")
+                )
+            else:
+                nc.scalar.copy(
+                    out=grouped1[:, d].bitcast(F32), in_=h1T[:].rearrange("p u n -> p n u")
+                )
+
+        h0_pairs = h0_sb[:].bitcast(F32)
+        h0T = psum.tile([P, S_PASSES, 2, P], F32, tag="bank")
+        for g in range(S_PASSES):
+            for u in range(2):
+                nc.tensor.transpose(
+                    h0T[:, g, u, :], h0_pairs[:, 256 * g + u : 256 * (g + 1) : 2], ident[:]
+                )
+        grouped0 = sb.tile([P, S_PASSES, P, 4], BF16, align_bytes=64)
+        nc.vector.tensor_copy(
+            out=grouped0[:].bitcast(F32), in_=h0T[:].rearrange("p g u n -> p g n u")
+        )
+        for d in (0, 2, 1):
+            nc.vector.quantize_mx(
+                out=q1_codes[:, d].bitcast(FP8X4),
+                scales=q1_scales[:, d],
+                in_=grouped1[:, d].rearrange("p n t -> p (n t)"),
+            )
+        q0_codes = sb.tile([P, S_PASSES, P], U32, align_bytes=64)
+        q0_scales = sb.tile([P, S_PASSES, P], U8, align_bytes=64)
+        nc.vector.quantize_mx(
+            out=q0_codes[:].rearrange("p g n -> p (g n)").bitcast(FP8X4),
+            scales=q0_scales[:].rearrange("p g n -> p (g n)"),
+            in_=grouped0[:].rearrange("p g n t -> p (g n t)"),
+        )
+
+        byp_v_sb = sb.tile([P, V_BLOCKS, DV, P], F32)
+        for b in range(V_BLOCKS):
+            byp_v = psum.tile([P, DV, P], F32, tag="bank")
+            for d in range(DV):
+                for a in range(2):
+                    j, e = divmod(DV * a + d, 2)
+                    nc.tensor.matmul(
+                        byp_v[:, d, :],
+                        lhsT=byp1_sb[:, a, b * P : (b + 1) * P],
+                        rhs=f1T_sb[:, j, :, e],
+                        start=(a == 0),
+                        stop=(a == 1),
+                    )
+            nc.scalar.activation(
+                out=byp_v_sb[:, b], in_=byp_v[:], func=ACT.Copy, scale=1.0 / math.sqrt(IN_V)
+            )
+        byp_s_sb = sb.tile([P, S_BLOCKS, P], F32)
+        nc.scalar.activation(out=byp_s_sb[:], in_=byp_s[:], func=ACT.Copy, scale=1.0 / math.sqrt(IN_S))
+
+        prm_f32 = sb.tile([P, P], F32)
+        nc.vector.tensor_copy(out=prm_f32[:], in_=prm_rows[:])
+        prmT = psum.tile([P, P], F32, tag="bank")
+        nc.tensor.transpose(prmT[:], prm_f32[:], ident[:])
+        prm = sb.tile([P, n_w + S_BLOCKS], F32)
+        nc.vector.tensor_copy(out=prm[:], in_=prmT[:, 0 : n_w + S_BLOCKS])
+        gain_s = prm[:, 0:S_BLOCKS]
+        gain_v = prm[:, S_BLOCKS:n_w]
+        bias_s = prm[:, n_w : n_w + S_BLOCKS]
+
+        y_v = sb.tile([P, V_BLOCKS, DV, P], F32)
+        squares = sb.tile([P, V_BLOCKS, DV, P], F32)
+        sumsq_v = sb.tile([P, V_BLOCKS], F32)
+        for b in range(V_BLOCKS):
+            lin_v = psum.tile([P, DV, P], F32, tag="bank")
+            for d in range(DV):
+                nc.tensor.matmul_mx(
+                    out=lin_v[:, d, :],
+                    lhsT=w1_words[:, 2 * b * P : 2 * (b + 1) * P].bitcast(FP4X4),
+                    lhsT_scale=w1_planes[:, 0, b * P : (b + 1) * P],
+                    rhs=q1_codes[:, d, :].bitcast(FP8X4),
+                    rhs_scale=q1_scales[:, d, :],
+                    start=True,
+                    stop=True,
+                )
+            nc.vector.scalar_tensor_tensor(
+                out=y_v[:, b].rearrange("o d n -> o (d n)"),
+                in0=lin_v[:].rearrange("o d n -> o (d n)"),
+                scalar=1.0 / math.sqrt(HID_V),
+                in1=byp_v_sb[:, b].rearrange("o d n -> o (d n)"),
+                op0=ALU.mult,
+                op1=ALU.add,
+            )
+            nc.scalar.activation(
+                out=squares[:, b], in_=y_v[:, b], func=ACT.Square, accum_out=sumsq_v[:, b : b + 1]
+            )
+        lin_s = psum.tile([P, S_BLOCKS, P], F32, tag="bank")
+        for b in range(S_BLOCKS):
+            for g in range(S_PASSES):
+                nc.tensor.matmul_mx(
+                    out=lin_s[:, b, :],
+                    lhsT=w0_words[:, g, 2 * b * P : 2 * (b + 1) * P].bitcast(FP4X4),
+                    lhsT_scale=w0_planes[:, g, b * P : (b + 1) * P],
+                    rhs=q0_codes[:, g, :].bitcast(FP8X4),
+                    rhs_scale=q0_scales[:, g, :],
+                    start=(g == 0),
+                    stop=(g == S_PASSES - 1),
+                )
+        y_s = sb.tile([P, S_BLOCKS, P], F32)
+        nc.vector.scalar_tensor_tensor(
+            out=y_s[:].rearrange("o b n -> o (b n)"),
+            in0=lin_s[:].rearrange("o b n -> o (b n)"),
+            scalar=1.0 / math.sqrt(HID_S),
+            in1=byp_s_sb[:].rearrange("o b n -> o (b n)"),
+            op0=ALU.mult,
+            op1=ALU.add,
+        )
+
+        out_sb = sb.tile([P, OUT_S + OUT_V * DV], F32)
+        scale_v = sb.tile([P, V_BLOCKS], F32)
+        nc.scalar.activation(
+            out=scale_v[:],
+            in_=sumsq_v[:],
+            func=ACT.Abs_reciprocal_sqrt,
+            scale=1.0 / (P * DV),
+            bias=EPS,
+        )
+        nc.vector.tensor_tensor(out=scale_v[:], in0=scale_v[:], in1=gain_v, op=ALU.mult)
+        z_v = sb.tile([P, V_BLOCKS, DV, P], F32)
+        for b in range(V_BLOCKS):
+            nc.scalar.mul(out=z_v[:, b], in_=y_v[:, b], mul=scale_v[:, b : b + 1])
+
+        stats = sb.tile([P, S_BLOCKS, 6], F32)
+        mean_var = sb.tile([P, S_BLOCKS, 2], F32)
+        for b in range(S_BLOCKS):
+            nc.vector.bn_stats(out=stats[:, b, :], in_=y_s[:, b, :])
+        for b in range(S_BLOCKS):
+            nc.vector.bn_aggr(out=mean_var[:, b, :], in_=stats[:, b, :])
+        scale_s = sb.tile([P, S_BLOCKS], F32)
+        nc.scalar.activation(
+            out=scale_s[:], in_=mean_var[:, :, 1], func=ACT.Abs_reciprocal_sqrt, bias=EPS
+        )
+        centred = sb.tile([P, S_BLOCKS, P], F32)
+        for b in range(S_BLOCKS):
+            nc.vector.tensor_scalar(
+                out=centred[:, b, :],
+                in0=y_s[:, b, :],
+                scalar1=mean_var[:, b, 0:1],
+                scalar2=None,
+                op0=ALU.subtract,
+            )
+        nc.vector.tensor_tensor(out=scale_s[:], in0=scale_s[:], in1=gain_s, op=ALU.mult)
+        z_s = sb.tile([P, S_BLOCKS, P], F32)
+        for b in range(S_BLOCKS):
+            nc.vector.tensor_scalar(
+                out=z_s[:, b, :],
+                in0=centred[:, b, :],
+                scalar1=scale_s[:, b : b + 1],
+                scalar2=bias_s[:, b : b + 1],
+                op0=ALU.mult,
+                op1=ALU.add,
+            )
+
+        for b in range(V_BLOCKS):
+            zT_v = psum.tile([P, DV, P], F32, tag="bank")
+            for d in range(DV):
+                nc.tensor.transpose(zT_v[:, d, :], z_v[:, b, d, :], ident[:])
+            cols = slice(OUT_S + b * P * DV, OUT_S + (b + 1) * P * DV)
+            nc.scalar.copy(
+                out=out_sb[:, cols].rearrange("n (o d) -> n o d", d=DV),
+                in_=zT_v[:].rearrange("n d o -> n o d"),
+            )
+            nc.sync.dma_start(out=out[:, cols], in_=out_sb[:, cols])
+        zT_s = psum.tile([P, S_BLOCKS, P], F32, tag="bank")
+        for b in range(S_BLOCKS):
+            nc.tensor.transpose(zT_s[:, b, :], z_s[:, b, :], ident[:])
+        nc.vector.tensor_copy(out=out_sb[:, :OUT_S], in_=zT_s[:].rearrange("n b o -> n (b o)"))
+        nc.sync.dma_start(out=out[:, :OUT_S], in_=out_sb[:, :OUT_S])

@@ -23,6 +23,7 @@ S_BLOCKS = OUT_S // P
 V_BLOCKS = OUT_V // P
 S_PASSES = HID_S // 512
 EPS = 1e-5
+WARM_UP_MATMULS = 5
 
 FLOPS = 2 * P * (HID_S * OUT_S + DV * HID_V * OUT_V + IN_S * OUT_S + DV * IN_V * OUT_V)
 
@@ -53,94 +54,80 @@ def tile_feedforward_pb_s_kernel(
                     in_=rows.bitcast(I32)[:, 4 * quad : 4 * quad + 4, :].rearrange("g r w -> r g w"),
                 )
 
+        zeros = sb.tile([P, P], F32)
+        nc.vector.memset(zeros[:], 0.0)
+        idle_ps = psum.tile([P, P], F32, tag="bank")
+        for i in range(WARM_UP_MATMULS):
+            nc.tensor.matmul(idle_ps[:], lhsT=zeros[:], rhs=zeros[:], start=True, stop=True)
         w1_planes = sb.tile([P, 1, OUT_V], U8, align_bytes=64)
         w0_planes = sb.tile([P, S_PASSES, OUT_S], U8, align_bytes=64)
         nc.vector.memset(w1_planes[:].bitcast(I32), 0)
+        ident = sb.tile([P, P], F32)
+        nc.vector.memset(ident[:], 0.0)
+        make_identity(nc, ident[:], nomemset=True)
+        warm = sb.tile([P, 1], F32)
+        nc.vector.memset(warm[:], 1.0)
         nc.vector.memset(w0_planes[:].bitcast(I32), 0)
         prm_rows = sb.tile([P, P], BF16)
         nc.vector.memset(prm_rows[:], 0.0)
-        warm = sb.tile([P, 1], F32)
-        nc.vector.memset(warm[:], 1.0)
-        ident = sb.tile([P, P], F32)
-        make_identity(nc, ident[:])
 
         load_scale_rows(w1_planes, lin3_W1_scales)
-        feat_sb = sb.tile([P, IN_S + IN_V * DV], BF16)
-        nc.scalar.dma_start(out=feat_sb[:], in_=features)
-        byp0_sb = sb.tile([P, 2, 2, OUT_S], BF16)
-        nc.scalar.dma_start(out=byp0_sb[:], in_=byp_W0.rearrange("(c p e) o -> p c e o", c=2, e=2))
         h1_sb = sb.tile([P, HID_V * DV], BF16)
         nc.scalar.dma_start(out=h1_sb[:], in_=h2[:, HID_S:])
-        h0_sb = sb.tile([P, HID_S], BF16)
-        nc.scalar.dma_start(out=h0_sb[:], in_=h2[:, :HID_S])
+        f1_sb = sb.tile([P, IN_V * DV], BF16)
+        nc.scalar.dma_start(out=f1_sb[:], in_=features[:, IN_S:])
+        byp1_sb = sb.tile([P, 2, OUT_V], BF16)
+        nc.scalar.dma_start(out=byp1_sb[:], in_=byp_W1.rearrange("(q a) o -> q a o", a=2))
         nc.scalar.activation(out=warm[:], in_=warm[:], func=ACT.Abs_reciprocal_sqrt)
         w1_words = sb.tile([P, 2 * OUT_V], U8, align_bytes=64)
         nc.sync.dma_start(out=w1_words[:].bitcast(I32), in_=lin3_W1_words[0].bitcast(I32))
+        h0_sb = sb.tile([P, HID_S], BF16)
+        nc.sync.dma_start(out=h0_sb[:], in_=h2[:, :HID_S])
+        f0_sb = sb.tile([P, IN_S], BF16)
+        nc.sync.dma_start(out=f0_sb[:], in_=features[:, :IN_S])
+        load_scale_rows(w0_planes, lin3_W0_scales)
+        byp0_sb = sb.tile([P, 2, 2, OUT_S], BF16)
+        byp0_rows = byp_W0.rearrange("(c p e) o -> c p e o", c=2, e=2)
+        for c in range(2):
+            nc.sync.dma_start(out=byp0_sb[:, c], in_=byp0_rows[c])
         w0_words = sb.tile([P, S_PASSES, 2 * OUT_S], U8, align_bytes=64)
         nc.sync.dma_start(
             out=w0_words[:].bitcast(I32), in_=lin3_W0_words.bitcast(I32).rearrange("g p w -> p g w")
         )
-        byp1_sb = sb.tile([P, 2, OUT_V], BF16)
-        nc.gpsimd.dma_start(out=byp1_sb[:], in_=byp_W1.rearrange("(q a) o -> q a o", a=2))
-        load_scale_rows(w0_planes, lin3_W0_scales)
         n_w = S_BLOCKS + V_BLOCKS
         nc.gpsimd.dma_start(out=prm_rows[0:n_w, :], in_=bn_weight.rearrange("(b o) -> b o", o=P))
         nc.gpsimd.dma_start(
             out=prm_rows[n_w : n_w + S_BLOCKS, :], in_=bn_bias.rearrange("(b o) -> b o", o=P)
         )
 
-        feat_pairs = feat_sb[:].bitcast(F32)
-        f0T = psum.tile([P, 2, P], F32, tag="bank")
-        for c in range(2):
-            nc.tensor.transpose(f0T[:, c, :], feat_pairs[:, c * P : (c + 1) * P], ident[:])
-        f1T = psum.tile([P, DV, P], F32, tag="bank")
-        for j in range(DV):
-            nc.tensor.transpose(f1T[:, j, :], feat_pairs[:, IN_S // 2 + j :: DV], ident[:])
-        f0T_sb = sb.tile([P, 2, P, 2], BF16)
-        nc.scalar.copy(
-            out=f0T_sb[:].rearrange("p c n e -> p (c n e)"),
-            in_=f0T[:].rearrange("p c n -> p (c n)").bitcast(BF16),
-        )
-        f1T_sb = sb.tile([P, DV, P, 2], BF16)
-        nc.vector.tensor_copy(
-            out=f1T_sb[:].rearrange("p j n e -> p (j n e)"),
-            in_=f1T[:].rearrange("p j n -> p (j n)").bitcast(BF16),
-        )
-
-        byp_s = psum.tile([P, S_BLOCKS, P], F32, tag="bank")
-        for b in range(S_BLOCKS):
-            for ce in range(4):
-                c, e = divmod(ce, 2)
-                nc.tensor.matmul(
-                    byp_s[:, b, :],
-                    lhsT=byp0_sb[:, c, e, b * P : (b + 1) * P],
-                    rhs=f0T_sb[:, c, :, e],
-                    start=(ce == 0),
-                    stop=(ce == 3),
-                )
 
         h1_sorted = sb.tile([P, DV, 2, P, 2], BF16)
         h1_by_d = h1_sb[:].rearrange("n (p u e d) -> n d u p e", u=2, e=2, d=DV)
         nc.vector.tensor_copy(out=h1_sorted[:, 0], in_=h1_by_d[:, 0])
         nc.scalar.copy(out=h1_sorted[:, 2], in_=h1_by_d[:, 2])
         nc.vector.tensor_copy(out=h1_sorted[:, 1], in_=h1_by_d[:, 1])
+
+        f1_pairs = f1_sb[:].bitcast(F32)
+        f1T = psum.tile([P, DV, P], F32, tag="bank")
+        for j in range(DV):
+            nc.tensor.transpose(f1T[:, j, :], f1_pairs[:, j::DV], ident[:])
+        f1T_sb = sb.tile([P, DV, P, 2], BF16)
+        nc.scalar.copy(
+            out=f1T_sb[:].rearrange("p j n e -> p (j n e)"),
+            in_=f1T[:].rearrange("p j n -> p (j n)").bitcast(BF16),
+        )
         grouped1 = sb.tile([P, DV, P, 4], BF16, align_bytes=64)
-        q1_codes = sb.tile([P, DV, P], U32, align_bytes=64)
-        q1_scales = sb.tile([P, DV, P], U8, align_bytes=64)
-        for d in (0, 2, 1):
+
+        def transpose_h1(d, copy):
             h1_pairs = h1_sorted[:, d].rearrange("n u p e -> n (u p e)").bitcast(F32)
-            h1T = psum.tile([P, 2, P], F32, tag="bank")
+            h1T = psum.tile([P, 2, P], F32, tag="bank", name="h1T")
             for u in range(2):
                 nc.tensor.transpose(h1T[:, u, :], h1_pairs[:, u * P : (u + 1) * P], ident[:])
-            if d == 0:
-                nc.vector.tensor_copy(
-                    out=grouped1[:, d].bitcast(F32), in_=h1T[:].rearrange("p u n -> p n u")
-                )
-            else:
-                nc.scalar.copy(
-                    out=grouped1[:, d].bitcast(F32), in_=h1T[:].rearrange("p u n -> p n u")
-                )
+            copy(out=grouped1[:, d].bitcast(F32), in_=h1T[:].rearrange("p u n -> p n u"))
 
+        transpose_h1(0, nc.vector.tensor_copy)
+        transpose_h1(2, nc.scalar.copy)
+        transpose_h1(1, nc.vector.tensor_copy)
         h0_pairs = h0_sb[:].bitcast(F32)
         h0T = psum.tile([P, S_PASSES, 2, P], F32, tag="bank")
         for g in range(S_PASSES):
@@ -148,15 +135,45 @@ def tile_feedforward_pb_s_kernel(
                 nc.tensor.transpose(
                     h0T[:, g, u, :], h0_pairs[:, 256 * g + u : 256 * (g + 1) : 2], ident[:]
                 )
-        grouped0 = sb.tile([P, S_PASSES, P, 4], BF16, align_bytes=64)
-        nc.vector.tensor_copy(
-            out=grouped0[:].bitcast(F32), in_=h0T[:].rearrange("p g u n -> p g n u")
-        )
+        f0_pairs = f0_sb[:].bitcast(F32)
+        f0T = psum.tile([P, 2, P], F32, tag="bank")
+        for c in range(2):
+            nc.tensor.transpose(f0T[:, c, :], f0_pairs[:, c * P : (c + 1) * P], ident[:])
+
+        q1_codes = sb.tile([P, DV, P], U32, align_bytes=64)
+        q1_scales = sb.tile([P, DV, P], U8, align_bytes=64)
         for d in (0, 2, 1):
             nc.vector.quantize_mx(
                 out=q1_codes[:, d].bitcast(FP8X4),
                 scales=q1_scales[:, d],
                 in_=grouped1[:, d].rearrange("p n t -> p (n t)"),
+            )
+
+        byp_v = [psum.tile([P, DV, P], F32, tag="bank", name="byp_v%d" % b) for b in range(V_BLOCKS)]
+        for b in range(V_BLOCKS):
+            for d in range(DV):
+                for a in range(2):
+                    j, e = divmod(DV * a + d, 2)
+                    nc.tensor.matmul(
+                        byp_v[b][:, d, :],
+                        lhsT=byp1_sb[:, a, b * P : (b + 1) * P],
+                        rhs=f1T_sb[:, j, :, e],
+                        start=(a == 0),
+                        stop=(a == 1),
+                    )
+        grouped0 = sb.tile([P, S_PASSES, P, 4], BF16, align_bytes=64)
+        nc.vector.tensor_copy(
+            out=grouped0[:].bitcast(F32), in_=h0T[:].rearrange("p g u n -> p g n u")
+        )
+        f0T_sb = sb.tile([P, 2, P, 2], BF16)
+        nc.scalar.copy(
+            out=f0T_sb[:].rearrange("p c n e -> p (c n e)"),
+            in_=f0T[:].rearrange("p c n -> p (c n)").bitcast(BF16),
+        )
+        byp_v_sb = sb.tile([P, V_BLOCKS, DV, P], F32)
+        for b in range(V_BLOCKS):
+            nc.scalar.activation(
+                out=byp_v_sb[:, b], in_=byp_v[b][:], func=ACT.Copy, scale=1.0 / math.sqrt(IN_V)
             )
         q0_codes = sb.tile([P, S_PASSES, P], U32, align_bytes=64)
         q0_scales = sb.tile([P, S_PASSES, P], U8, align_bytes=64)
@@ -166,24 +183,46 @@ def tile_feedforward_pb_s_kernel(
             in_=grouped0[:].rearrange("p g n t -> p (g n t)"),
         )
 
-        byp_v_sb = sb.tile([P, V_BLOCKS, DV, P], F32)
+        lin_v = [psum.tile([P, DV, P], F32, tag="bank", name="lin_v%d" % b) for b in range(V_BLOCKS)]
         for b in range(V_BLOCKS):
-            byp_v = psum.tile([P, DV, P], F32, tag="bank")
             for d in range(DV):
-                for a in range(2):
-                    j, e = divmod(DV * a + d, 2)
+                nc.tensor.matmul_mx(
+                    out=lin_v[b][:, d, :],
+                    lhsT=w1_words[:, 2 * b * P : 2 * (b + 1) * P].bitcast(FP4X4),
+                    lhsT_scale=w1_planes[:, 0, b * P : (b + 1) * P],
+                    rhs=q1_codes[:, d, :].bitcast(FP8X4),
+                    rhs_scale=q1_scales[:, d, :],
+                    start=True,
+                    stop=True,
+                )
+
+        byp_s = [psum.tile([P, P], F32, tag="bank", name="byp_s%d" % b) for b in range(S_BLOCKS)]
+        for c in range(2):
+            for b in range(S_BLOCKS):
+                for e in range(2):
                     nc.tensor.matmul(
-                        byp_v[:, d, :],
-                        lhsT=byp1_sb[:, a, b * P : (b + 1) * P],
-                        rhs=f1T_sb[:, j, :, e],
-                        start=(a == 0),
-                        stop=(a == 1),
+                        byp_s[b][:],
+                        lhsT=byp0_sb[:, c, e, b * P : (b + 1) * P],
+                        rhs=f0T_sb[:, c, :, e],
+                        start=(c == 0 and e == 0),
+                        stop=(c == 1 and e == 1),
                     )
-            nc.scalar.activation(
-                out=byp_v_sb[:, b], in_=byp_v[:], func=ACT.Copy, scale=1.0 / math.sqrt(IN_V)
+
+        y_v = sb.tile([P, V_BLOCKS, DV, P], F32)
+        squares = sb.tile([P, V_BLOCKS, DV, P], F32)
+        sumsq_v = sb.tile([P, V_BLOCKS], F32)
+        for b in range(V_BLOCKS):
+            nc.vector.scalar_tensor_tensor(
+                out=y_v[:, b].rearrange("o d n -> o (d n)"),
+                in0=lin_v[b][:].rearrange("o d n -> o (d n)"),
+                scalar=1.0 / math.sqrt(HID_V),
+                in1=byp_v_sb[:, b].rearrange("o d n -> o (d n)"),
+                op0=ALU.mult,
+                op1=ALU.add,
             )
-        byp_s_sb = sb.tile([P, S_BLOCKS, P], F32)
-        nc.scalar.activation(out=byp_s_sb[:], in_=byp_s[:], func=ACT.Copy, scale=1.0 / math.sqrt(IN_S))
+            nc.scalar.activation(
+                out=squares[:, b], in_=y_v[:, b], func=ACT.Square, accum_out=sumsq_v[:, b : b + 1]
+            )
 
         prm_f32 = sb.tile([P, P], F32)
         nc.vector.tensor_copy(out=prm_f32[:], in_=prm_rows[:])
@@ -195,32 +234,6 @@ def tile_feedforward_pb_s_kernel(
         gain_v = prm[:, S_BLOCKS:n_w]
         bias_s = prm[:, n_w : n_w + S_BLOCKS]
 
-        y_v = sb.tile([P, V_BLOCKS, DV, P], F32)
-        squares = sb.tile([P, V_BLOCKS, DV, P], F32)
-        sumsq_v = sb.tile([P, V_BLOCKS], F32)
-        for b in range(V_BLOCKS):
-            lin_v = psum.tile([P, DV, P], F32, tag="bank")
-            for d in range(DV):
-                nc.tensor.matmul_mx(
-                    out=lin_v[:, d, :],
-                    lhsT=w1_words[:, 2 * b * P : 2 * (b + 1) * P].bitcast(FP4X4),
-                    lhsT_scale=w1_planes[:, 0, b * P : (b + 1) * P],
-                    rhs=q1_codes[:, d, :].bitcast(FP8X4),
-                    rhs_scale=q1_scales[:, d, :],
-                    start=True,
-                    stop=True,
-                )
-            nc.vector.scalar_tensor_tensor(
-                out=y_v[:, b].rearrange("o d n -> o (d n)"),
-                in0=lin_v[:].rearrange("o d n -> o (d n)"),
-                scalar=1.0 / math.sqrt(HID_V),
-                in1=byp_v_sb[:, b].rearrange("o d n -> o (d n)"),
-                op0=ALU.mult,
-                op1=ALU.add,
-            )
-            nc.scalar.activation(
-                out=squares[:, b], in_=y_v[:, b], func=ACT.Square, accum_out=sumsq_v[:, b : b + 1]
-            )
         lin_s = psum.tile([P, S_BLOCKS, P], F32, tag="bank")
         for b in range(S_BLOCKS):
             for g in range(S_PASSES):
@@ -233,6 +246,21 @@ def tile_feedforward_pb_s_kernel(
                     start=(g == 0),
                     stop=(g == S_PASSES - 1),
                 )
+        byp_s_sb = sb.tile([P, S_BLOCKS, P], F32)
+        for b in range(S_BLOCKS):
+            nc.scalar.activation(
+                out=byp_s_sb[:, b, :], in_=byp_s[b][:], func=ACT.Copy, scale=1.0 / math.sqrt(IN_S)
+            )
+
+        out_sb = sb.tile([P, OUT_S + OUT_V * DV], F32)
+        rstd_v = sb.tile([P, V_BLOCKS], F32)
+        nc.scalar.activation(
+            out=rstd_v[:],
+            in_=sumsq_v[:],
+            func=ACT.Abs_reciprocal_sqrt,
+            scale=1.0 / (P * DV),
+            bias=EPS,
+        )
         y_s = sb.tile([P, S_BLOCKS, P], F32)
         nc.vector.scalar_tensor_tensor(
             out=y_s[:].rearrange("o b n -> o (b n)"),
@@ -242,64 +270,57 @@ def tile_feedforward_pb_s_kernel(
             op0=ALU.mult,
             op1=ALU.add,
         )
-
-        out_sb = sb.tile([P, OUT_S + OUT_V * DV], F32)
-        scale_v = sb.tile([P, V_BLOCKS], F32)
-        nc.scalar.activation(
-            out=scale_v[:],
-            in_=sumsq_v[:],
-            func=ACT.Abs_reciprocal_sqrt,
-            scale=1.0 / (P * DV),
-            bias=EPS,
-        )
-        nc.vector.tensor_tensor(out=scale_v[:], in0=scale_v[:], in1=gain_v, op=ALU.mult)
-        z_v = sb.tile([P, V_BLOCKS, DV, P], F32)
-        for b in range(V_BLOCKS):
-            nc.scalar.mul(out=z_v[:, b], in_=y_v[:, b], mul=scale_v[:, b : b + 1])
-
         stats = sb.tile([P, S_BLOCKS, 6], F32)
         mean_var = sb.tile([P, S_BLOCKS, 2], F32)
         for b in range(S_BLOCKS):
             nc.vector.bn_stats(out=stats[:, b, :], in_=y_s[:, b, :])
+        scale_v = sb.tile([P, V_BLOCKS], F32)
+        nc.vector.tensor_tensor(out=scale_v[:], in0=rstd_v[:], in1=gain_v, op=ALU.mult)
         for b in range(S_BLOCKS):
             nc.vector.bn_aggr(out=mean_var[:, b, :], in_=stats[:, b, :])
-        scale_s = sb.tile([P, S_BLOCKS], F32)
+
+        z_v = sb.tile([P, V_BLOCKS, DV, P], F32)
+        zT_v = [psum.tile([P, DV, P], F32, tag="bank", name="zT_v%d" % b) for b in range(V_BLOCKS)]
+
+        def scale_and_transpose_vectors(b):
+            nc.scalar.mul(out=z_v[:, b], in_=y_v[:, b], mul=scale_v[:, b : b + 1])
+            for d in range(DV):
+                nc.tensor.transpose(zT_v[b][:, d, :], z_v[:, b, d, :], ident[:])
+
+        scale_and_transpose_vectors(0)
+        rstd_s = sb.tile([P, S_BLOCKS], F32)
         nc.scalar.activation(
-            out=scale_s[:], in_=mean_var[:, :, 1], func=ACT.Abs_reciprocal_sqrt, bias=EPS
+            out=rstd_s[:], in_=mean_var[:, :, 1], func=ACT.Abs_reciprocal_sqrt, bias=EPS
         )
+        scale_and_transpose_vectors(1)
         centred = sb.tile([P, S_BLOCKS, P], F32)
         for b in range(S_BLOCKS):
             nc.vector.tensor_scalar(
                 out=centred[:, b, :],
                 in0=y_s[:, b, :],
                 scalar1=mean_var[:, b, 0:1],
-                scalar2=None,
+                scalar2=gain_s[:, b : b + 1],
                 op0=ALU.subtract,
+                op1=ALU.mult,
             )
-        nc.vector.tensor_tensor(out=scale_s[:], in0=scale_s[:], in1=gain_s, op=ALU.mult)
         z_s = sb.tile([P, S_BLOCKS, P], F32)
+        zT_s = psum.tile([P, S_BLOCKS, P], F32, tag="bank")
         for b in range(S_BLOCKS):
             nc.vector.tensor_scalar(
                 out=z_s[:, b, :],
                 in0=centred[:, b, :],
-                scalar1=scale_s[:, b : b + 1],
+                scalar1=rstd_s[:, b : b + 1],
                 scalar2=bias_s[:, b : b + 1],
                 op0=ALU.mult,
                 op1=ALU.add,
             )
-
+            nc.tensor.transpose(zT_s[:, b, :], z_s[:, b, :], ident[:])
         for b in range(V_BLOCKS):
-            zT_v = psum.tile([P, DV, P], F32, tag="bank")
-            for d in range(DV):
-                nc.tensor.transpose(zT_v[:, d, :], z_v[:, b, d, :], ident[:])
             cols = slice(OUT_S + b * P * DV, OUT_S + (b + 1) * P * DV)
             nc.scalar.copy(
                 out=out_sb[:, cols].rearrange("n (o d) -> n o d", d=DV),
-                in_=zT_v[:].rearrange("n d o -> n o d"),
+                in_=zT_v[b][:].rearrange("n d o -> n o d"),
             )
             nc.sync.dma_start(out=out[:, cols], in_=out_sb[:, cols])
-        zT_s = psum.tile([P, S_BLOCKS, P], F32, tag="bank")
-        for b in range(S_BLOCKS):
-            nc.tensor.transpose(zT_s[:, b, :], z_s[:, b, :], ident[:])
         nc.vector.tensor_copy(out=out_sb[:, :OUT_S], in_=zT_s[:].rearrange("n b o -> n (b o)"))
         nc.sync.dma_start(out=out[:, :OUT_S], in_=out_sb[:, :OUT_S])

@@ -46,6 +46,7 @@ def tile_feedforward_pb_s_kernel(
     with ExitStack() as ctx:
         sb = ctx.enter_context(tc.tile_pool(name="sb", bufs=1))
         psum = ctx.enter_context(tc.psum_pool(name="psum", bufs=8))
+        ctx.enter_context(tc.manual_schedule())
 
         def load_scale_rows(planes, rows):
             for quad in range(4):
@@ -67,9 +68,9 @@ def tile_feedforward_pb_s_kernel(
         make_identity(nc, ident[:], nomemset=True)
         warm = sb.tile([P, 1], F32)
         nc.vector.memset(warm[:], 1.0)
-        nc.vector.memset(w0_planes[:].bitcast(I32), 0)
         prm_rows = sb.tile([P, P], BF16)
         nc.vector.memset(prm_rows[:], 0.0)
+        nc.vector.memset(w0_planes[:].bitcast(I32), 0)
 
         load_scale_rows(w1_planes, lin3_W1_scales)
         h1_sb = sb.tile([P, HID_V * DV], BF16)
@@ -81,25 +82,22 @@ def tile_feedforward_pb_s_kernel(
         nc.scalar.activation(out=warm[:], in_=warm[:], func=ACT.Abs_reciprocal_sqrt)
         w1_words = sb.tile([P, 2 * OUT_V], U8, align_bytes=64)
         nc.sync.dma_start(out=w1_words[:].bitcast(I32), in_=lin3_W1_words[0].bitcast(I32))
+        n_w = S_BLOCKS + V_BLOCKS
+        nc.sync.dma_start(out=prm_rows[0:n_w, :], in_=bn_weight.rearrange("(b o) -> b o", o=P))
+        nc.sync.dma_start(
+            out=prm_rows[n_w : n_w + S_BLOCKS, :], in_=bn_bias.rearrange("(b o) -> b o", o=P)
+        )
         h0_sb = sb.tile([P, HID_S], BF16)
         nc.sync.dma_start(out=h0_sb[:], in_=h2[:, :HID_S])
         f0_sb = sb.tile([P, IN_S], BF16)
         nc.sync.dma_start(out=f0_sb[:], in_=features[:, :IN_S])
-        load_scale_rows(w0_planes, lin3_W0_scales)
         byp0_sb = sb.tile([P, 2, 2, OUT_S], BF16)
-        byp0_rows = byp_W0.rearrange("(c p e) o -> c p e o", c=2, e=2)
-        for c in range(2):
-            nc.sync.dma_start(out=byp0_sb[:, c], in_=byp0_rows[c])
+        nc.sync.dma_start(out=byp0_sb[:], in_=byp_W0.rearrange("(c p e) o -> p c e o", c=2, e=2))
+        load_scale_rows(w0_planes, lin3_W0_scales)
         w0_words = sb.tile([P, S_PASSES, 2 * OUT_S], U8, align_bytes=64)
         nc.sync.dma_start(
             out=w0_words[:].bitcast(I32), in_=lin3_W0_words.bitcast(I32).rearrange("g p w -> p g w")
         )
-        n_w = S_BLOCKS + V_BLOCKS
-        nc.gpsimd.dma_start(out=prm_rows[0:n_w, :], in_=bn_weight.rearrange("(b o) -> b o", o=P))
-        nc.gpsimd.dma_start(
-            out=prm_rows[n_w : n_w + S_BLOCKS, :], in_=bn_bias.rearrange("(b o) -> b o", o=P)
-        )
-
 
         h1_sorted = sb.tile([P, DV, 2, P, 2], BF16)
         h1_by_d = h1_sb[:].rearrange("n (p u e d) -> n d u p e", u=2, e=2, d=DV)
@@ -116,6 +114,8 @@ def tile_feedforward_pb_s_kernel(
             out=f1T_sb[:].rearrange("p j n e -> p (j n e)"),
             in_=f1T[:].rearrange("p j n -> p (j n)").bitcast(BF16),
         )
+        prm_f32 = sb.tile([P, P], F32)
+        nc.vector.tensor_copy(out=prm_f32[:], in_=prm_rows[:])
         grouped1 = sb.tile([P, DV, P, 4], BF16, align_bytes=64)
 
         def transpose_h1(d, copy):
@@ -128,6 +128,8 @@ def tile_feedforward_pb_s_kernel(
         transpose_h1(0, nc.vector.tensor_copy)
         transpose_h1(2, nc.scalar.copy)
         transpose_h1(1, nc.vector.tensor_copy)
+        prmT = psum.tile([P, P], F32, tag="bank")
+        nc.tensor.transpose(prmT[:], prm_f32[:], ident[:])
         h0_pairs = h0_sb[:].bitcast(F32)
         h0T = psum.tile([P, S_PASSES, 2, P], F32, tag="bank")
         for g in range(S_PASSES):
@@ -148,19 +150,11 @@ def tile_feedforward_pb_s_kernel(
                 scales=q1_scales[:, d],
                 in_=grouped1[:, d].rearrange("p n t -> p (n t)"),
             )
-
-        byp_v = [psum.tile([P, DV, P], F32, tag="bank", name="byp_v%d" % b) for b in range(V_BLOCKS)]
-        for b in range(V_BLOCKS):
-            for d in range(DV):
-                for a in range(2):
-                    j, e = divmod(DV * a + d, 2)
-                    nc.tensor.matmul(
-                        byp_v[b][:, d, :],
-                        lhsT=byp1_sb[:, a, b * P : (b + 1) * P],
-                        rhs=f1T_sb[:, j, :, e],
-                        start=(a == 0),
-                        stop=(a == 1),
-                    )
+        prm = sb.tile([P, n_w + S_BLOCKS], F32)
+        nc.vector.tensor_copy(out=prm[:], in_=prmT[:, 0 : n_w + S_BLOCKS])
+        gain_s = prm[:, 0:S_BLOCKS]
+        gain_v = prm[:, S_BLOCKS:n_w]
+        bias_s = prm[:, n_w : n_w + S_BLOCKS]
         grouped0 = sb.tile([P, S_PASSES, P, 4], BF16, align_bytes=64)
         nc.vector.tensor_copy(
             out=grouped0[:].bitcast(F32), in_=h0T[:].rearrange("p g u n -> p g n u")
@@ -170,11 +164,6 @@ def tile_feedforward_pb_s_kernel(
             out=f0T_sb[:].rearrange("p c n e -> p (c n e)"),
             in_=f0T[:].rearrange("p c n -> p (c n)").bitcast(BF16),
         )
-        byp_v_sb = sb.tile([P, V_BLOCKS, DV, P], F32)
-        for b in range(V_BLOCKS):
-            nc.scalar.activation(
-                out=byp_v_sb[:, b], in_=byp_v[b][:], func=ACT.Copy, scale=1.0 / math.sqrt(IN_V)
-            )
         q0_codes = sb.tile([P, S_PASSES, P], U32, align_bytes=64)
         q0_scales = sb.tile([P, S_PASSES, P], U8, align_bytes=64)
         nc.vector.quantize_mx(
@@ -183,8 +172,43 @@ def tile_feedforward_pb_s_kernel(
             in_=grouped0[:].rearrange("p g n t -> p (g n t)"),
         )
 
-        lin_v = [psum.tile([P, DV, P], F32, tag="bank", name="lin_v%d" % b) for b in range(V_BLOCKS)]
-        for b in range(V_BLOCKS):
+        byp_v_sb = sb.tile([P, V_BLOCKS, DV, P], F32)
+        y_v = sb.tile([P, V_BLOCKS, DV, P], F32)
+        squares = sb.tile([P, V_BLOCKS, DV, P], F32)
+        sumsq_v = sb.tile([P, V_BLOCKS], F32)
+        rstd_v = sb.tile([P, V_BLOCKS], F32)
+        z_v = sb.tile([P, V_BLOCKS, DV, P], F32)
+        byp_s_sb = sb.tile([P, S_BLOCKS, P], F32)
+        y_s = sb.tile([P, S_BLOCKS, P], F32)
+        stats = sb.tile([P, S_BLOCKS, 6], F32)
+        mean_var = sb.tile([P, S_BLOCKS, 2], F32)
+        rstd_s = sb.tile([P, S_BLOCKS], F32)
+        centred = sb.tile([P, S_BLOCKS, P], F32)
+        z_s = sb.tile([P, S_BLOCKS, P], F32)
+        out_sb = sb.tile([P, OUT_S + OUT_V * DV], F32)
+        lin_v = {}
+        lin_s = {}
+        zT_v = {}
+        zT_s = {}
+
+        def bypass_vectors(b):
+            byp = psum.tile([P, DV, P], F32, tag="bank", name="byp_v")
+            for d in range(DV):
+                for a in range(2):
+                    j, e = divmod(DV * a + d, 2)
+                    nc.tensor.matmul(
+                        byp[:, d, :],
+                        lhsT=byp1_sb[:, a, b * P : (b + 1) * P],
+                        rhs=f1T_sb[:, j, :, e],
+                        start=(a == 0),
+                        stop=(a == 1),
+                    )
+            nc.scalar.activation(
+                out=byp_v_sb[:, b], in_=byp[:], func=ACT.Copy, scale=1.0 / math.sqrt(IN_V)
+            )
+
+        def linear_vectors(b):
+            lin_v[b] = psum.tile([P, DV, P], F32, tag="bank", name="lin_v")
             for d in range(DV):
                 nc.tensor.matmul_mx(
                     out=lin_v[b][:, d, :],
@@ -196,22 +220,7 @@ def tile_feedforward_pb_s_kernel(
                     stop=True,
                 )
 
-        byp_s = [psum.tile([P, P], F32, tag="bank", name="byp_s%d" % b) for b in range(S_BLOCKS)]
-        for c in range(2):
-            for b in range(S_BLOCKS):
-                for e in range(2):
-                    nc.tensor.matmul(
-                        byp_s[b][:],
-                        lhsT=byp0_sb[:, c, e, b * P : (b + 1) * P],
-                        rhs=f0T_sb[:, c, :, e],
-                        start=(c == 0 and e == 0),
-                        stop=(c == 1 and e == 1),
-                    )
-
-        y_v = sb.tile([P, V_BLOCKS, DV, P], F32)
-        squares = sb.tile([P, V_BLOCKS, DV, P], F32)
-        sumsq_v = sb.tile([P, V_BLOCKS], F32)
-        for b in range(V_BLOCKS):
+        def sum_vectors(b):
             nc.vector.scalar_tensor_tensor(
                 out=y_v[:, b].rearrange("o d n -> o (d n)"),
                 in0=lin_v[b][:].rearrange("o d n -> o (d n)"),
@@ -220,25 +229,53 @@ def tile_feedforward_pb_s_kernel(
                 op0=ALU.mult,
                 op1=ALU.add,
             )
+
+        def sum_of_squares_vectors(b):
             nc.scalar.activation(
                 out=squares[:, b], in_=y_v[:, b], func=ACT.Square, accum_out=sumsq_v[:, b : b + 1]
             )
 
-        prm_f32 = sb.tile([P, P], F32)
-        nc.vector.tensor_copy(out=prm_f32[:], in_=prm_rows[:])
-        prmT = psum.tile([P, P], F32, tag="bank")
-        nc.tensor.transpose(prmT[:], prm_f32[:], ident[:])
-        prm = sb.tile([P, n_w + S_BLOCKS], F32)
-        nc.vector.tensor_copy(out=prm[:], in_=prmT[:, 0 : n_w + S_BLOCKS])
-        gain_s = prm[:, 0:S_BLOCKS]
-        gain_v = prm[:, S_BLOCKS:n_w]
-        bias_s = prm[:, n_w : n_w + S_BLOCKS]
+        def normalise_vectors(b):
+            nc.vector.tensor_scalar(
+                out=z_v[:, b],
+                in0=y_v[:, b],
+                scalar1=rstd_v[:, b : b + 1],
+                scalar2=gain_v[:, b : b + 1],
+                op0=ALU.mult,
+                op1=ALU.mult,
+            )
+            zT_v[b] = psum.tile([P, DV, P], F32, tag="bank", name="zT_v")
+            for d in range(DV):
+                nc.tensor.transpose(zT_v[b][:, d, :], z_v[:, b, d, :], ident[:])
 
-        lin_s = psum.tile([P, S_BLOCKS, P], F32, tag="bank")
-        for b in range(S_BLOCKS):
+        def store_vectors(b):
+            cols = slice(OUT_S + b * P * DV, OUT_S + (b + 1) * P * DV)
+            nc.scalar.copy(
+                out=out_sb[:, cols].rearrange("n (o d) -> n o d", d=DV),
+                in_=zT_v[b][:].rearrange("n d o -> n o d"),
+            )
+            nc.sync.dma_start(out=out[:, cols], in_=out_sb[:, cols])
+
+        def bypass_scalars(b):
+            byp = psum.tile([P, P], F32, tag="bank", name="byp_s")
+            for ce in range(4):
+                c, e = divmod(ce, 2)
+                nc.tensor.matmul(
+                    byp[:],
+                    lhsT=byp0_sb[:, c, e, b * P : (b + 1) * P],
+                    rhs=f0T_sb[:, c, :, e],
+                    start=(ce == 0),
+                    stop=(ce == 3),
+                )
+            nc.scalar.activation(
+                out=byp_s_sb[:, b, :], in_=byp[:], func=ACT.Copy, scale=1.0 / math.sqrt(IN_S)
+            )
+
+        def linear_scalars(b):
+            lin_s[b] = psum.tile([P, P], F32, tag="bank", name="lin_s")
             for g in range(S_PASSES):
                 nc.tensor.matmul_mx(
-                    out=lin_s[:, b, :],
+                    out=lin_s[b][:],
                     lhsT=w0_words[:, g, 2 * b * P : 2 * (b + 1) * P].bitcast(FP4X4),
                     lhsT_scale=w0_planes[:, g, b * P : (b + 1) * P],
                     rhs=q0_codes[:, g, :].bitcast(FP8X4),
@@ -246,55 +283,27 @@ def tile_feedforward_pb_s_kernel(
                     start=(g == 0),
                     stop=(g == S_PASSES - 1),
                 )
-        byp_s_sb = sb.tile([P, S_BLOCKS, P], F32)
-        for b in range(S_BLOCKS):
-            nc.scalar.activation(
-                out=byp_s_sb[:, b, :], in_=byp_s[b][:], func=ACT.Copy, scale=1.0 / math.sqrt(IN_S)
+
+        def sum_scalars(b):
+            nc.vector.scalar_tensor_tensor(
+                out=y_s[:, b, :],
+                in0=lin_s[b][:],
+                scalar=1.0 / math.sqrt(HID_S),
+                in1=byp_s_sb[:, b, :],
+                op0=ALU.mult,
+                op1=ALU.add,
             )
 
-        out_sb = sb.tile([P, OUT_S + OUT_V * DV], F32)
-        rstd_v = sb.tile([P, V_BLOCKS], F32)
-        nc.scalar.activation(
-            out=rstd_v[:],
-            in_=sumsq_v[:],
-            func=ACT.Abs_reciprocal_sqrt,
-            scale=1.0 / (P * DV),
-            bias=EPS,
-        )
-        y_s = sb.tile([P, S_BLOCKS, P], F32)
-        nc.vector.scalar_tensor_tensor(
-            out=y_s[:].rearrange("o b n -> o (b n)"),
-            in0=lin_s[:].rearrange("o b n -> o (b n)"),
-            scalar=1.0 / math.sqrt(HID_S),
-            in1=byp_s_sb[:].rearrange("o b n -> o (b n)"),
-            op0=ALU.mult,
-            op1=ALU.add,
-        )
-        stats = sb.tile([P, S_BLOCKS, 6], F32)
-        mean_var = sb.tile([P, S_BLOCKS, 2], F32)
-        for b in range(S_BLOCKS):
-            nc.vector.bn_stats(out=stats[:, b, :], in_=y_s[:, b, :])
-        scale_v = sb.tile([P, V_BLOCKS], F32)
-        nc.vector.tensor_tensor(out=scale_v[:], in0=rstd_v[:], in1=gain_v, op=ALU.mult)
-        for b in range(S_BLOCKS):
+        def mean_and_rstd_scalars(b):
             nc.vector.bn_aggr(out=mean_var[:, b, :], in_=stats[:, b, :])
+            nc.scalar.activation(
+                out=rstd_s[:, b : b + 1],
+                in_=mean_var[:, b, 1:2],
+                func=ACT.Abs_reciprocal_sqrt,
+                bias=EPS,
+            )
 
-        z_v = sb.tile([P, V_BLOCKS, DV, P], F32)
-        zT_v = [psum.tile([P, DV, P], F32, tag="bank", name="zT_v%d" % b) for b in range(V_BLOCKS)]
-
-        def scale_and_transpose_vectors(b):
-            nc.scalar.mul(out=z_v[:, b], in_=y_v[:, b], mul=scale_v[:, b : b + 1])
-            for d in range(DV):
-                nc.tensor.transpose(zT_v[b][:, d, :], z_v[:, b, d, :], ident[:])
-
-        scale_and_transpose_vectors(0)
-        rstd_s = sb.tile([P, S_BLOCKS], F32)
-        nc.scalar.activation(
-            out=rstd_s[:], in_=mean_var[:, :, 1], func=ACT.Abs_reciprocal_sqrt, bias=EPS
-        )
-        scale_and_transpose_vectors(1)
-        centred = sb.tile([P, S_BLOCKS, P], F32)
-        for b in range(S_BLOCKS):
+        def centre_scalars(b):
             nc.vector.tensor_scalar(
                 out=centred[:, b, :],
                 in0=y_s[:, b, :],
@@ -303,24 +312,61 @@ def tile_feedforward_pb_s_kernel(
                 op0=ALU.subtract,
                 op1=ALU.mult,
             )
-        z_s = sb.tile([P, S_BLOCKS, P], F32)
-        zT_s = psum.tile([P, S_BLOCKS, P], F32, tag="bank")
-        for b in range(S_BLOCKS):
-            nc.vector.tensor_scalar(
+
+        def normalise_scalars(b):
+            nc.scalar.activation(
                 out=z_s[:, b, :],
-                in0=centred[:, b, :],
-                scalar1=rstd_s[:, b : b + 1],
-                scalar2=bias_s[:, b : b + 1],
-                op0=ALU.mult,
-                op1=ALU.add,
+                in_=centred[:, b, :],
+                func=ACT.Identity,
+                scale=rstd_s[:, b : b + 1],
+                bias=bias_s[:, b : b + 1],
             )
-            nc.tensor.transpose(zT_s[:, b, :], z_s[:, b, :], ident[:])
-        for b in range(V_BLOCKS):
-            cols = slice(OUT_S + b * P * DV, OUT_S + (b + 1) * P * DV)
-            nc.scalar.copy(
-                out=out_sb[:, cols].rearrange("n (o d) -> n o d", d=DV),
-                in_=zT_v[b][:].rearrange("n d o -> n o d"),
-            )
+            zT_s[b] = psum.tile([P, P], F32, tag="bank", name="zT_s")
+            nc.tensor.transpose(zT_s[b][:], z_s[:, b, :], ident[:])
+
+        def store_scalars(b):
+            cols = slice(b * P, (b + 1) * P)
+            nc.vector.tensor_copy(out=out_sb[:, cols], in_=zT_s[b][:])
             nc.sync.dma_start(out=out[:, cols], in_=out_sb[:, cols])
-        nc.vector.tensor_copy(out=out_sb[:, :OUT_S], in_=zT_s[:].rearrange("n b o -> n (b o)"))
-        nc.sync.dma_start(out=out[:, :OUT_S], in_=out_sb[:, :OUT_S])
+
+        for b in range(V_BLOCKS):
+            bypass_vectors(b)
+        for b in range(V_BLOCKS):
+            linear_vectors(b)
+        bypass_scalars(0)
+        bypass_scalars(1)
+        linear_scalars(0)
+        for b in range(V_BLOCKS):
+            sum_vectors(b)
+
+        for i in range(S_BLOCKS + 3):
+            if i < V_BLOCKS:
+                sum_of_squares_vectors(i)
+            if i + 2 < S_BLOCKS:
+                bypass_scalars(i + 2)
+            if i + 1 < S_BLOCKS:
+                linear_scalars(i + 1)
+            if i < S_BLOCKS:
+                sum_scalars(i)
+            if 0 <= i - 1 < S_BLOCKS:
+                mean_and_rstd_scalars(i - 1)
+            if i < S_BLOCKS:
+                nc.vector.bn_stats(out=stats[:, i, :], in_=y_s[:, i, :])
+            if 0 <= i - 1 < S_BLOCKS:
+                centre_scalars(i - 1)
+            if i == V_BLOCKS:
+                nc.scalar.activation(
+                    out=rstd_v[:],
+                    in_=sumsq_v[:],
+                    func=ACT.Abs_reciprocal_sqrt,
+                    scale=1.0 / (P * DV),
+                    bias=EPS,
+                )
+            if 0 <= i - 2 < S_BLOCKS:
+                normalise_scalars(i - 2)
+            if 0 <= i - 3 < V_BLOCKS:
+                normalise_vectors(i - 3)
+            if 0 <= i - 3 < S_BLOCKS:
+                store_scalars(i - 3)
+            if 0 <= i - 5 < V_BLOCKS:
+                store_vectors(i - 5)

@@ -23,7 +23,7 @@ S_BLOCKS = OUT_S // P
 V_BLOCKS = OUT_V // P
 S_PASSES = HID_S // 512
 EPS = 1e-5
-WARM_UP_MATMULS = 5
+WARM_UP_MATMULS = 3
 
 FLOPS = 2 * P * (HID_S * OUT_S + DV * HID_V * OUT_V + IN_S * OUT_S + DV * IN_V * OUT_V)
 
@@ -46,7 +46,6 @@ def tile_feedforward_pb_s_kernel(
     with ExitStack() as ctx:
         sb = ctx.enter_context(tc.tile_pool(name="sb", bufs=1))
         psum = ctx.enter_context(tc.psum_pool(name="psum", bufs=8))
-        ctx.enter_context(tc.manual_schedule())
 
         def load_scale_rows(planes, rows):
             for quad in range(4):
@@ -68,42 +67,39 @@ def tile_feedforward_pb_s_kernel(
         make_identity(nc, ident[:], nomemset=True)
         warm = sb.tile([P, 1], F32)
         nc.vector.memset(warm[:], 1.0)
+        nc.vector.memset(w0_planes[:].bitcast(I32), 0)
         prm_rows = sb.tile([P, P], BF16)
         nc.vector.memset(prm_rows[:], 0.0)
-        nc.vector.memset(w0_planes[:].bitcast(I32), 0)
 
         load_scale_rows(w1_planes, lin3_W1_scales)
-        h1_sb = sb.tile([P, HID_V * DV], BF16)
-        nc.scalar.dma_start(out=h1_sb[:], in_=h2[:, HID_S:])
         f1_sb = sb.tile([P, IN_V * DV], BF16)
         nc.scalar.dma_start(out=f1_sb[:], in_=features[:, IN_S:])
+        h1_sb = sb.tile([P, HID_V * DV], BF16)
+        nc.scalar.dma_start(out=h1_sb[:], in_=h2[:, HID_S:])
         byp1_sb = sb.tile([P, 2, OUT_V], BF16)
         nc.scalar.dma_start(out=byp1_sb[:], in_=byp_W1.rearrange("(q a) o -> q a o", a=2))
         nc.scalar.activation(out=warm[:], in_=warm[:], func=ACT.Abs_reciprocal_sqrt)
         w1_words = sb.tile([P, 2 * OUT_V], U8, align_bytes=64)
         nc.sync.dma_start(out=w1_words[:].bitcast(I32), in_=lin3_W1_words[0].bitcast(I32))
-        n_w = S_BLOCKS + V_BLOCKS
-        nc.sync.dma_start(out=prm_rows[0:n_w, :], in_=bn_weight.rearrange("(b o) -> b o", o=P))
-        nc.sync.dma_start(
-            out=prm_rows[n_w : n_w + S_BLOCKS, :], in_=bn_bias.rearrange("(b o) -> b o", o=P)
-        )
         h0_sb = sb.tile([P, HID_S], BF16)
         nc.sync.dma_start(out=h0_sb[:], in_=h2[:, :HID_S])
         f0_sb = sb.tile([P, IN_S], BF16)
         nc.sync.dma_start(out=f0_sb[:], in_=features[:, :IN_S])
-        byp0_sb = sb.tile([P, 2, 2, OUT_S], BF16)
-        nc.sync.dma_start(out=byp0_sb[:], in_=byp_W0.rearrange("(c p e) o -> p c e o", c=2, e=2))
         load_scale_rows(w0_planes, lin3_W0_scales)
+        byp0_sb = sb.tile([P, 2, 2, OUT_S], BF16)
+        byp0_rows = byp_W0.rearrange("(c p e) o -> c p e o", c=2, e=2)
+        for c in range(2):
+            nc.sync.dma_start(out=byp0_sb[:, c], in_=byp0_rows[c])
         w0_words = sb.tile([P, S_PASSES, 2 * OUT_S], U8, align_bytes=64)
         nc.sync.dma_start(
             out=w0_words[:].bitcast(I32), in_=lin3_W0_words.bitcast(I32).rearrange("g p w -> p g w")
         )
+        n_w = S_BLOCKS + V_BLOCKS
+        nc.gpsimd.dma_start(out=prm_rows[0:n_w, :], in_=bn_weight.rearrange("(b o) -> b o", o=P))
+        nc.gpsimd.dma_start(
+            out=prm_rows[n_w : n_w + S_BLOCKS, :], in_=bn_bias.rearrange("(b o) -> b o", o=P)
+        )
 
-        h1_sorted = sb.tile([P, DV, 2, P, 2], BF16)
-        h1_by_d = h1_sb[:].rearrange("n (p u e d) -> n d u p e", u=2, e=2, d=DV)
-        nc.vector.tensor_copy(out=h1_sorted[:, 0], in_=h1_by_d[:, 0])
-        nc.scalar.copy(out=h1_sorted[:, 2], in_=h1_by_d[:, 2])
-        nc.vector.tensor_copy(out=h1_sorted[:, 1], in_=h1_by_d[:, 1])
 
         f1_pairs = f1_sb[:].bitcast(F32)
         f1T = psum.tile([P, DV, P], F32, tag="bank")
@@ -114,8 +110,12 @@ def tile_feedforward_pb_s_kernel(
             out=f1T_sb[:].rearrange("p j n e -> p (j n e)"),
             in_=f1T[:].rearrange("p j n -> p (j n)").bitcast(BF16),
         )
-        prm_f32 = sb.tile([P, P], F32)
-        nc.vector.tensor_copy(out=prm_f32[:], in_=prm_rows[:])
+        h1_sorted = sb.tile([P, DV, 2, P, 2], BF16)
+        h1_by_d = h1_sb[:].rearrange("n (p u e d) -> n d u p e", u=2, e=2, d=DV)
+        nc.vector.tensor_copy(out=h1_sorted[:, 0], in_=h1_by_d[:, 0])
+        nc.scalar.copy(out=h1_sorted[:, 2], in_=h1_by_d[:, 2])
+        nc.vector.tensor_copy(out=h1_sorted[:, 1], in_=h1_by_d[:, 1])
+
         grouped1 = sb.tile([P, DV, P, 4], BF16, align_bytes=64)
 
         def transpose_h1(d, copy):
@@ -128,8 +128,6 @@ def tile_feedforward_pb_s_kernel(
         transpose_h1(0, nc.vector.tensor_copy)
         transpose_h1(2, nc.scalar.copy)
         transpose_h1(1, nc.vector.tensor_copy)
-        prmT = psum.tile([P, P], F32, tag="bank")
-        nc.tensor.transpose(prmT[:], prm_f32[:], ident[:])
         h0_pairs = h0_sb[:].bitcast(F32)
         h0T = psum.tile([P, S_PASSES, 2, P], F32, tag="bank")
         for g in range(S_PASSES):
@@ -150,11 +148,19 @@ def tile_feedforward_pb_s_kernel(
                 scales=q1_scales[:, d],
                 in_=grouped1[:, d].rearrange("p n t -> p (n t)"),
             )
-        prm = sb.tile([P, n_w + S_BLOCKS], F32)
-        nc.vector.tensor_copy(out=prm[:], in_=prmT[:, 0 : n_w + S_BLOCKS])
-        gain_s = prm[:, 0:S_BLOCKS]
-        gain_v = prm[:, S_BLOCKS:n_w]
-        bias_s = prm[:, n_w : n_w + S_BLOCKS]
+
+        byp_v = [psum.tile([P, DV, P], F32, tag="bank", name="byp_v%d" % b) for b in range(V_BLOCKS)]
+        for b in range(V_BLOCKS):
+            for d in range(DV):
+                for a in range(2):
+                    j, e = divmod(DV * a + d, 2)
+                    nc.tensor.matmul(
+                        byp_v[b][:, d, :],
+                        lhsT=byp1_sb[:, a, b * P : (b + 1) * P],
+                        rhs=f1T_sb[:, j, :, e],
+                        start=(a == 0),
+                        stop=(a == 1),
+                    )
         grouped0 = sb.tile([P, S_PASSES, P, 4], BF16, align_bytes=64)
         nc.vector.tensor_copy(
             out=grouped0[:].bitcast(F32), in_=h0T[:].rearrange("p g u n -> p g n u")
@@ -164,6 +170,11 @@ def tile_feedforward_pb_s_kernel(
             out=f0T_sb[:].rearrange("p c n e -> p (c n e)"),
             in_=f0T[:].rearrange("p c n -> p (c n)").bitcast(BF16),
         )
+        byp_v_sb = sb.tile([P, V_BLOCKS, DV, P], F32)
+        for b in range(V_BLOCKS):
+            nc.scalar.activation(
+                out=byp_v_sb[:, b], in_=byp_v[b][:], func=ACT.Copy, scale=1.0 / math.sqrt(IN_V)
+            )
         q0_codes = sb.tile([P, S_PASSES, P], U32, align_bytes=64)
         q0_scales = sb.tile([P, S_PASSES, P], U8, align_bytes=64)
         nc.vector.quantize_mx(
@@ -172,43 +183,8 @@ def tile_feedforward_pb_s_kernel(
             in_=grouped0[:].rearrange("p g n t -> p (g n t)"),
         )
 
-        byp_v_sb = sb.tile([P, V_BLOCKS, DV, P], F32)
-        y_v = sb.tile([P, V_BLOCKS, DV, P], F32)
-        squares = sb.tile([P, V_BLOCKS, DV, P], F32)
-        sumsq_v = sb.tile([P, V_BLOCKS], F32)
-        rstd_v = sb.tile([P, V_BLOCKS], F32)
-        z_v = sb.tile([P, V_BLOCKS, DV, P], F32)
-        byp_s_sb = sb.tile([P, S_BLOCKS, P], F32)
-        y_s = sb.tile([P, S_BLOCKS, P], F32)
-        stats = sb.tile([P, S_BLOCKS, 6], F32)
-        mean_var = sb.tile([P, S_BLOCKS, 2], F32)
-        rstd_s = sb.tile([P, S_BLOCKS], F32)
-        centred = sb.tile([P, S_BLOCKS, P], F32)
-        z_s = sb.tile([P, S_BLOCKS, P], F32)
-        out_sb = sb.tile([P, OUT_S + OUT_V * DV], F32)
-        lin_v = {}
-        lin_s = {}
-        zT_v = {}
-        zT_s = {}
-
-        def bypass_vectors(b):
-            byp = psum.tile([P, DV, P], F32, tag="bank", name="byp_v")
-            for d in range(DV):
-                for a in range(2):
-                    j, e = divmod(DV * a + d, 2)
-                    nc.tensor.matmul(
-                        byp[:, d, :],
-                        lhsT=byp1_sb[:, a, b * P : (b + 1) * P],
-                        rhs=f1T_sb[:, j, :, e],
-                        start=(a == 0),
-                        stop=(a == 1),
-                    )
-            nc.scalar.activation(
-                out=byp_v_sb[:, b], in_=byp[:], func=ACT.Copy, scale=1.0 / math.sqrt(IN_V)
-            )
-
-        def linear_vectors(b):
-            lin_v[b] = psum.tile([P, DV, P], F32, tag="bank", name="lin_v")
+        lin_v = [psum.tile([P, DV, P], F32, tag="bank", name="lin_v%d" % b) for b in range(V_BLOCKS)]
+        for b in range(V_BLOCKS):
             for d in range(DV):
                 nc.tensor.matmul_mx(
                     out=lin_v[b][:, d, :],
@@ -220,7 +196,22 @@ def tile_feedforward_pb_s_kernel(
                     stop=True,
                 )
 
-        def sum_vectors(b):
+        byp_s = [psum.tile([P, P], F32, tag="bank", name="byp_s%d" % b) for b in range(S_BLOCKS)]
+        for c in range(2):
+            for b in range(S_BLOCKS):
+                for e in range(2):
+                    nc.tensor.matmul(
+                        byp_s[b][:],
+                        lhsT=byp0_sb[:, c, e, b * P : (b + 1) * P],
+                        rhs=f0T_sb[:, c, :, e],
+                        start=(c == 0 and e == 0),
+                        stop=(c == 1 and e == 1),
+                    )
+
+        y_v = sb.tile([P, V_BLOCKS, DV, P], F32)
+        squares = sb.tile([P, V_BLOCKS, DV, P], F32)
+        sumsq_v = sb.tile([P, V_BLOCKS], F32)
+        for b in range(V_BLOCKS):
             nc.vector.scalar_tensor_tensor(
                 out=y_v[:, b].rearrange("o d n -> o (d n)"),
                 in0=lin_v[b][:].rearrange("o d n -> o (d n)"),
@@ -229,53 +220,25 @@ def tile_feedforward_pb_s_kernel(
                 op0=ALU.mult,
                 op1=ALU.add,
             )
-
-        def sum_of_squares_vectors(b):
             nc.scalar.activation(
                 out=squares[:, b], in_=y_v[:, b], func=ACT.Square, accum_out=sumsq_v[:, b : b + 1]
             )
 
-        def normalise_vectors(b):
-            nc.vector.tensor_scalar(
-                out=z_v[:, b],
-                in0=y_v[:, b],
-                scalar1=rstd_v[:, b : b + 1],
-                scalar2=gain_v[:, b : b + 1],
-                op0=ALU.mult,
-                op1=ALU.mult,
-            )
-            zT_v[b] = psum.tile([P, DV, P], F32, tag="bank", name="zT_v")
-            for d in range(DV):
-                nc.tensor.transpose(zT_v[b][:, d, :], z_v[:, b, d, :], ident[:])
+        prm_f32 = sb.tile([P, P], F32)
+        nc.vector.tensor_copy(out=prm_f32[:], in_=prm_rows[:])
+        prmT = psum.tile([P, P], F32, tag="bank")
+        nc.tensor.transpose(prmT[:], prm_f32[:], ident[:])
+        prm = sb.tile([P, n_w + S_BLOCKS], F32)
+        nc.vector.tensor_copy(out=prm[:], in_=prmT[:, 0 : n_w + S_BLOCKS])
+        gain_s = prm[:, 0:S_BLOCKS]
+        gain_v = prm[:, S_BLOCKS:n_w]
+        bias_s = prm[:, n_w : n_w + S_BLOCKS]
 
-        def store_vectors(b):
-            cols = slice(OUT_S + b * P * DV, OUT_S + (b + 1) * P * DV)
-            nc.scalar.copy(
-                out=out_sb[:, cols].rearrange("n (o d) -> n o d", d=DV),
-                in_=zT_v[b][:].rearrange("n d o -> n o d"),
-            )
-            nc.sync.dma_start(out=out[:, cols], in_=out_sb[:, cols])
-
-        def bypass_scalars(b):
-            byp = psum.tile([P, P], F32, tag="bank", name="byp_s")
-            for ce in range(4):
-                c, e = divmod(ce, 2)
-                nc.tensor.matmul(
-                    byp[:],
-                    lhsT=byp0_sb[:, c, e, b * P : (b + 1) * P],
-                    rhs=f0T_sb[:, c, :, e],
-                    start=(ce == 0),
-                    stop=(ce == 3),
-                )
-            nc.scalar.activation(
-                out=byp_s_sb[:, b, :], in_=byp[:], func=ACT.Copy, scale=1.0 / math.sqrt(IN_S)
-            )
-
-        def linear_scalars(b):
-            lin_s[b] = psum.tile([P, P], F32, tag="bank", name="lin_s")
+        lin_s = psum.tile([P, S_BLOCKS, P], F32, tag="bank")
+        for b in range(S_BLOCKS):
             for g in range(S_PASSES):
                 nc.tensor.matmul_mx(
-                    out=lin_s[b][:],
+                    out=lin_s[:, b, :],
                     lhsT=w0_words[:, g, 2 * b * P : 2 * (b + 1) * P].bitcast(FP4X4),
                     lhsT_scale=w0_planes[:, g, b * P : (b + 1) * P],
                     rhs=q0_codes[:, g, :].bitcast(FP8X4),
@@ -283,27 +246,55 @@ def tile_feedforward_pb_s_kernel(
                     start=(g == 0),
                     stop=(g == S_PASSES - 1),
                 )
-
-        def sum_scalars(b):
-            nc.vector.scalar_tensor_tensor(
-                out=y_s[:, b, :],
-                in0=lin_s[b][:],
-                scalar=1.0 / math.sqrt(HID_S),
-                in1=byp_s_sb[:, b, :],
-                op0=ALU.mult,
-                op1=ALU.add,
-            )
-
-        def mean_and_rstd_scalars(b):
-            nc.vector.bn_aggr(out=mean_var[:, b, :], in_=stats[:, b, :])
+        byp_s_sb = sb.tile([P, S_BLOCKS, P], F32)
+        for b in range(S_BLOCKS):
             nc.scalar.activation(
-                out=rstd_s[:, b : b + 1],
-                in_=mean_var[:, b, 1:2],
-                func=ACT.Abs_reciprocal_sqrt,
-                bias=EPS,
+                out=byp_s_sb[:, b, :], in_=byp_s[b][:], func=ACT.Copy, scale=1.0 / math.sqrt(IN_S)
             )
 
-        def centre_scalars(b):
+        out_sb = sb.tile([P, OUT_S + OUT_V * DV], F32)
+        rstd_v = sb.tile([P, V_BLOCKS], F32)
+        nc.scalar.activation(
+            out=rstd_v[:],
+            in_=sumsq_v[:],
+            func=ACT.Abs_reciprocal_sqrt,
+            scale=1.0 / (P * DV),
+            bias=EPS,
+        )
+        y_s = sb.tile([P, S_BLOCKS, P], F32)
+        nc.vector.scalar_tensor_tensor(
+            out=y_s[:].rearrange("o b n -> o (b n)"),
+            in0=lin_s[:].rearrange("o b n -> o (b n)"),
+            scalar=1.0 / math.sqrt(HID_S),
+            in1=byp_s_sb[:].rearrange("o b n -> o (b n)"),
+            op0=ALU.mult,
+            op1=ALU.add,
+        )
+        stats = sb.tile([P, S_BLOCKS, 6], F32)
+        mean_var = sb.tile([P, S_BLOCKS, 2], F32)
+        for b in range(S_BLOCKS):
+            nc.vector.bn_stats(out=stats[:, b, :], in_=y_s[:, b, :])
+        scale_v = sb.tile([P, V_BLOCKS], F32)
+        nc.vector.tensor_tensor(out=scale_v[:], in0=rstd_v[:], in1=gain_v, op=ALU.mult)
+        for b in range(S_BLOCKS):
+            nc.vector.bn_aggr(out=mean_var[:, b, :], in_=stats[:, b, :])
+
+        z_v = sb.tile([P, V_BLOCKS, DV, P], F32)
+        zT_v = [psum.tile([P, DV, P], F32, tag="bank", name="zT_v%d" % b) for b in range(V_BLOCKS)]
+
+        def scale_and_transpose_vectors(b):
+            nc.scalar.mul(out=z_v[:, b], in_=y_v[:, b], mul=scale_v[:, b : b + 1])
+            for d in range(DV):
+                nc.tensor.transpose(zT_v[b][:, d, :], z_v[:, b, d, :], ident[:])
+
+        scale_and_transpose_vectors(0)
+        rstd_s = sb.tile([P, S_BLOCKS], F32)
+        nc.scalar.activation(
+            out=rstd_s[:], in_=mean_var[:, :, 1], func=ACT.Abs_reciprocal_sqrt, bias=EPS
+        )
+        scale_and_transpose_vectors(1)
+        centred = sb.tile([P, S_BLOCKS, P], F32)
+        for b in range(S_BLOCKS):
             nc.vector.tensor_scalar(
                 out=centred[:, b, :],
                 in0=y_s[:, b, :],
@@ -312,61 +303,28 @@ def tile_feedforward_pb_s_kernel(
                 op0=ALU.subtract,
                 op1=ALU.mult,
             )
-
-        def normalise_scalars(b):
-            nc.scalar.activation(
+        z_s = sb.tile([P, S_BLOCKS, P], F32)
+        zT_s = [psum.tile([P, 2, P], F32, tag="bank", name="zT_s%d" % half) for half in range(2)]
+        for b in range(S_BLOCKS):
+            nc.vector.tensor_scalar(
                 out=z_s[:, b, :],
-                in_=centred[:, b, :],
-                func=ACT.Identity,
-                scale=rstd_s[:, b : b + 1],
-                bias=bias_s[:, b : b + 1],
+                in0=centred[:, b, :],
+                scalar1=rstd_s[:, b : b + 1],
+                scalar2=bias_s[:, b : b + 1],
+                op0=ALU.mult,
+                op1=ALU.add,
             )
-            zT_s[b] = psum.tile([P, P], F32, tag="bank", name="zT_s")
-            nc.tensor.transpose(zT_s[b][:], z_s[:, b, :], ident[:])
-
-        def store_scalars(b):
-            cols = slice(b * P, (b + 1) * P)
-            nc.vector.tensor_copy(out=out_sb[:, cols], in_=zT_s[b][:])
+            nc.tensor.transpose(zT_s[b // 2][:, b % 2, :], z_s[:, b, :], ident[:])
+        for b in range(V_BLOCKS):
+            cols = slice(OUT_S + b * P * DV, OUT_S + (b + 1) * P * DV)
+            nc.scalar.copy(
+                out=out_sb[:, cols].rearrange("n (o d) -> n o d", d=DV),
+                in_=zT_v[b][:].rearrange("n d o -> n o d"),
+            )
             nc.sync.dma_start(out=out[:, cols], in_=out_sb[:, cols])
-
-        for b in range(V_BLOCKS):
-            bypass_vectors(b)
-        for b in range(V_BLOCKS):
-            linear_vectors(b)
-        bypass_scalars(0)
-        bypass_scalars(1)
-        linear_scalars(0)
-        for b in range(V_BLOCKS):
-            sum_vectors(b)
-
-        for i in range(S_BLOCKS + 3):
-            if i < V_BLOCKS:
-                sum_of_squares_vectors(i)
-            if i + 2 < S_BLOCKS:
-                bypass_scalars(i + 2)
-            if i + 1 < S_BLOCKS:
-                linear_scalars(i + 1)
-            if i < S_BLOCKS:
-                sum_scalars(i)
-            if 0 <= i - 1 < S_BLOCKS:
-                mean_and_rstd_scalars(i - 1)
-            if i < S_BLOCKS:
-                nc.vector.bn_stats(out=stats[:, i, :], in_=y_s[:, i, :])
-            if 0 <= i - 1 < S_BLOCKS:
-                centre_scalars(i - 1)
-            if i == V_BLOCKS:
-                nc.scalar.activation(
-                    out=rstd_v[:],
-                    in_=sumsq_v[:],
-                    func=ACT.Abs_reciprocal_sqrt,
-                    scale=1.0 / (P * DV),
-                    bias=EPS,
-                )
-            if 0 <= i - 2 < S_BLOCKS:
-                normalise_scalars(i - 2)
-            if 0 <= i - 3 < V_BLOCKS:
-                normalise_vectors(i - 3)
-            if 0 <= i - 3 < S_BLOCKS:
-                store_scalars(i - 3)
-            if 0 <= i - 5 < V_BLOCKS:
-                store_vectors(i - 5)
+        nc.scalar.copy(out=out_sb[:, 0 : 2 * P], in_=zT_s[0][:].rearrange("n b o -> n (b o)"))
+        nc.sync.dma_start(out=out[:, 0 : 2 * P], in_=out_sb[:, 0 : 2 * P])
+        nc.vector.tensor_copy(
+            out=out_sb[:, 2 * P : 4 * P], in_=zT_s[1][:].rearrange("n b o -> n (b o)")
+        )
+        nc.sync.dma_start(out=out[:, 2 * P : 4 * P], in_=out_sb[:, 2 * P : 4 * P])

@@ -45,7 +45,10 @@ def tile_feedforward_pb_s_kernel(
     nc = tc.nc
     with ExitStack() as ctx:
         sb = ctx.enter_context(tc.tile_pool(name="sb", bufs=1))
-        psum = ctx.enter_context(tc.psum_pool(name="psum", bufs=8))
+        psum = ctx.enter_context(tc.psum_pool(name="psum", bufs=1))
+
+        def bank(i, shape, name):
+            return psum.tile(shape, F32, tag="bank%d" % i, name=name)
 
         def load_scale_rows(planes, rows):
             for quad in range(4):
@@ -54,62 +57,62 @@ def tile_feedforward_pb_s_kernel(
                     in_=rows.bitcast(I32)[:, 4 * quad : 4 * quad + 4, :].rearrange("g r w -> r g w"),
                 )
 
+        w1_planes = sb.tile([P, 1, OUT_V], U8, align_bytes=64)
+        nc.vector.memset(w1_planes[:].bitcast(I32), 0)
         zeros = sb.tile([P, P], F32)
         nc.vector.memset(zeros[:], 0.0)
-        idle_ps = psum.tile([P, P], F32, tag="bank")
+        idle_ps = bank(0, [P, P], "idle_ps")
         for i in range(WARM_UP_MATMULS):
             nc.tensor.matmul(idle_ps[:], lhsT=zeros[:], rhs=zeros[:], start=True, stop=True)
-        w1_planes = sb.tile([P, 1, OUT_V], U8, align_bytes=64)
         w0_planes = sb.tile([P, S_PASSES, OUT_S], U8, align_bytes=64)
-        nc.vector.memset(w1_planes[:].bitcast(I32), 0)
         ident = sb.tile([P, P], F32)
         nc.vector.memset(ident[:], 0.0)
         make_identity(nc, ident[:], nomemset=True)
         warm = sb.tile([P, 1], F32)
         nc.vector.memset(warm[:], 1.0)
         nc.vector.memset(w0_planes[:].bitcast(I32), 0)
-        prm_rows = sb.tile([P, P], BF16)
-        nc.vector.memset(prm_rows[:], 0.0)
+        gain_rows = sb.tile([P, P], BF16)
+        nc.vector.memset(gain_rows[:], 0.0)
+        bias_rows = sb.tile([P, P], BF16)
+        nc.vector.memset(bias_rows[:], 0.0)
 
-        load_scale_rows(w1_planes, lin3_W1_scales)
         f1_sb = sb.tile([P, IN_V * DV], BF16)
         nc.scalar.dma_start(out=f1_sb[:], in_=features[:, IN_S:])
-        h1_sb = sb.tile([P, HID_V * DV], BF16)
-        nc.scalar.dma_start(out=h1_sb[:], in_=h2[:, HID_S:])
-        byp1_sb = sb.tile([P, 2, OUT_V], BF16)
-        nc.scalar.dma_start(out=byp1_sb[:], in_=byp_W1.rearrange("(q a) o -> q a o", a=2))
         nc.scalar.activation(out=warm[:], in_=warm[:], func=ACT.Abs_reciprocal_sqrt)
-        w1_words = sb.tile([P, 2 * OUT_V], U8, align_bytes=64)
-        nc.sync.dma_start(out=w1_words[:].bitcast(I32), in_=lin3_W1_words[0].bitcast(I32))
+        load_scale_rows(w1_planes, lin3_W1_scales)
+        h1_sb = sb.tile([P, HID_V * DV], BF16)
+        nc.sync.dma_start(out=h1_sb[:], in_=h2[:, HID_S:])
+        byp1_sb = sb.tile([P, 2, OUT_V], BF16)
+        nc.sync.dma_start(out=byp1_sb[:], in_=byp_W1.rearrange("(q a) o -> q a o", a=2))
         h0_sb = sb.tile([P, HID_S], BF16)
         nc.sync.dma_start(out=h0_sb[:], in_=h2[:, :HID_S])
+        w1_words = sb.tile([P, 2 * OUT_V], U8, align_bytes=64)
+        nc.sync.dma_start(out=w1_words[:].bitcast(I32), in_=lin3_W1_words[0].bitcast(I32))
         f0_sb = sb.tile([P, IN_S], BF16)
         nc.sync.dma_start(out=f0_sb[:], in_=features[:, :IN_S])
-        load_scale_rows(w0_planes, lin3_W0_scales)
-        byp0_sb = sb.tile([P, 2, 2, OUT_S], BF16)
-        byp0_rows = byp_W0.rearrange("(c p e) o -> c p e o", c=2, e=2)
-        for c in range(2):
-            nc.sync.dma_start(out=byp0_sb[:, c], in_=byp0_rows[c])
         w0_words = sb.tile([P, S_PASSES, 2 * OUT_S], U8, align_bytes=64)
         nc.sync.dma_start(
             out=w0_words[:].bitcast(I32), in_=lin3_W0_words.bitcast(I32).rearrange("g p w -> p g w")
         )
+        byp0_sb = sb.tile([P, 2, 2, OUT_S], BF16)
+        byp0_rows = byp_W0.rearrange("(c p e) o -> c p e o", c=2, e=2)
+        for c in range(2):
+            nc.sync.dma_start(out=byp0_sb[:, c], in_=byp0_rows[c])
+        load_scale_rows(w0_planes, lin3_W0_scales)
         n_w = S_BLOCKS + V_BLOCKS
-        nc.gpsimd.dma_start(out=prm_rows[0:n_w, :], in_=bn_weight.rearrange("(b o) -> b o", o=P))
-        nc.gpsimd.dma_start(
-            out=prm_rows[n_w : n_w + S_BLOCKS, :], in_=bn_bias.rearrange("(b o) -> b o", o=P)
-        )
-
+        nc.gpsimd.dma_start(out=gain_rows[0:n_w, :], in_=bn_weight.rearrange("(b o) -> b o", o=P))
+        nc.gpsimd.dma_start(out=bias_rows[0:S_BLOCKS, :], in_=bn_bias.rearrange("(b o) -> b o", o=P))
 
         f1_pairs = f1_sb[:].bitcast(F32)
-        f1T = psum.tile([P, DV, P], F32, tag="bank")
+        f1T = bank(4, [P, DV, P], "f1T")
         for j in range(DV):
             nc.tensor.transpose(f1T[:, j, :], f1_pairs[:, j::DV], ident[:])
         f1T_sb = sb.tile([P, DV, P, 2], BF16)
         nc.scalar.copy(
-            out=f1T_sb[:].rearrange("p j n e -> p (j n e)"),
-            in_=f1T[:].rearrange("p j n -> p (j n)").bitcast(BF16),
+            out=f1T_sb[:].rearrange("p j n e -> p (j n e)").bitcast(F32),
+            in_=f1T[:].rearrange("p j n -> p (j n)"),
         )
+
         h1_sorted = sb.tile([P, DV, 2, P, 2], BF16)
         h1_by_d = h1_sb[:].rearrange("n (p u e d) -> n d u p e", u=2, e=2, d=DV)
         nc.vector.tensor_copy(out=h1_sorted[:, 0], in_=h1_by_d[:, 0])
@@ -117,39 +120,22 @@ def tile_feedforward_pb_s_kernel(
         nc.vector.tensor_copy(out=h1_sorted[:, 1], in_=h1_by_d[:, 1])
 
         grouped1 = sb.tile([P, DV, P, 4], BF16, align_bytes=64)
-
-        def transpose_h1(d, copy):
+        q1_codes = sb.tile([P, DV, P], U32, align_bytes=64)
+        q1_scales = sb.tile([P, DV, P], U8, align_bytes=64)
+        for d, copy in ((0, nc.vector.tensor_copy), (1, nc.scalar.copy), (2, nc.scalar.copy)):
             h1_pairs = h1_sorted[:, d].rearrange("n u p e -> n (u p e)").bitcast(F32)
-            h1T = psum.tile([P, 2, P], F32, tag="bank", name="h1T")
+            h1T = bank(1 + d, [P, 2, P], "h1T%d" % d)
             for u in range(2):
                 nc.tensor.transpose(h1T[:, u, :], h1_pairs[:, u * P : (u + 1) * P], ident[:])
             copy(out=grouped1[:, d].bitcast(F32), in_=h1T[:].rearrange("p u n -> p n u"))
-
-        transpose_h1(0, nc.vector.tensor_copy)
-        transpose_h1(2, nc.scalar.copy)
-        transpose_h1(1, nc.vector.tensor_copy)
-        h0_pairs = h0_sb[:].bitcast(F32)
-        h0T = psum.tile([P, S_PASSES, 2, P], F32, tag="bank")
-        for g in range(S_PASSES):
-            for u in range(2):
-                nc.tensor.transpose(
-                    h0T[:, g, u, :], h0_pairs[:, 256 * g + u : 256 * (g + 1) : 2], ident[:]
-                )
-        f0_pairs = f0_sb[:].bitcast(F32)
-        f0T = psum.tile([P, 2, P], F32, tag="bank")
-        for c in range(2):
-            nc.tensor.transpose(f0T[:, c, :], f0_pairs[:, c * P : (c + 1) * P], ident[:])
-
-        q1_codes = sb.tile([P, DV, P], U32, align_bytes=64)
-        q1_scales = sb.tile([P, DV, P], U8, align_bytes=64)
-        for d in (0, 2, 1):
+        for d in range(DV):
             nc.vector.quantize_mx(
                 out=q1_codes[:, d].bitcast(FP8X4),
                 scales=q1_scales[:, d],
                 in_=grouped1[:, d].rearrange("p n t -> p (n t)"),
             )
 
-        byp_v = [psum.tile([P, DV, P], F32, tag="bank", name="byp_v%d" % b) for b in range(V_BLOCKS)]
+        byp_v = [bank(5 + b, [P, DV, P], "byp_v%d" % b) for b in range(V_BLOCKS)]
         for b in range(V_BLOCKS):
             for d in range(DV):
                 for a in range(2):
@@ -161,20 +147,16 @@ def tile_feedforward_pb_s_kernel(
                         start=(a == 0),
                         stop=(a == 1),
                     )
+
+        h0_pairs = h0_sb[:].bitcast(F32)
+        h0T = bank(0, [P, S_PASSES, 2, P], "h0T")
+        for g in range(S_PASSES):
+            for u in range(2):
+                nc.tensor.transpose(
+                    h0T[:, g, u, :], h0_pairs[:, 256 * g + u : 256 * (g + 1) : 2], ident[:]
+                )
         grouped0 = sb.tile([P, S_PASSES, P, 4], BF16, align_bytes=64)
-        nc.vector.tensor_copy(
-            out=grouped0[:].bitcast(F32), in_=h0T[:].rearrange("p g u n -> p g n u")
-        )
-        f0T_sb = sb.tile([P, 2, P, 2], BF16)
-        nc.scalar.copy(
-            out=f0T_sb[:].rearrange("p c n e -> p (c n e)"),
-            in_=f0T[:].rearrange("p c n -> p (c n)").bitcast(BF16),
-        )
-        byp_v_sb = sb.tile([P, V_BLOCKS, DV, P], F32)
-        for b in range(V_BLOCKS):
-            nc.scalar.activation(
-                out=byp_v_sb[:, b], in_=byp_v[b][:], func=ACT.Copy, scale=1.0 / math.sqrt(IN_V)
-            )
+        nc.scalar.copy(out=grouped0[:].bitcast(F32), in_=h0T[:].rearrange("p g u n -> p g n u"))
         q0_codes = sb.tile([P, S_PASSES, P], U32, align_bytes=64)
         q0_scales = sb.tile([P, S_PASSES, P], U8, align_bytes=64)
         nc.vector.quantize_mx(
@@ -183,7 +165,22 @@ def tile_feedforward_pb_s_kernel(
             in_=grouped0[:].rearrange("p g n t -> p (g n t)"),
         )
 
-        lin_v = [psum.tile([P, DV, P], F32, tag="bank", name="lin_v%d" % b) for b in range(V_BLOCKS)]
+        f0_pairs = f0_sb[:].bitcast(F32)
+        f0T = bank(7, [P, 2, P], "f0T")
+        for c in range(2):
+            nc.tensor.transpose(f0T[:, c, :], f0_pairs[:, c * P : (c + 1) * P], ident[:])
+        f0T_sb = sb.tile([P, 2, P, 2], BF16)
+        nc.vector.tensor_copy(
+            out=f0T_sb[:].rearrange("p c n e -> p (c n e)").bitcast(F32),
+            in_=f0T[:].rearrange("p c n -> p (c n)"),
+        )
+
+        byp_v_sb = sb.tile([P, V_BLOCKS, DV, P], F32)
+        for b in range(V_BLOCKS):
+            nc.scalar.activation(
+                out=byp_v_sb[:, b], in_=byp_v[b][:], func=ACT.Copy, scale=1.0 / math.sqrt(IN_V)
+            )
+        lin_v = [bank(1 + b, [P, DV, P], "lin_v%d" % b) for b in range(V_BLOCKS)]
         for b in range(V_BLOCKS):
             for d in range(DV):
                 nc.tensor.matmul_mx(
@@ -196,17 +193,18 @@ def tile_feedforward_pb_s_kernel(
                     stop=True,
                 )
 
-        byp_s = [psum.tile([P, P], F32, tag="bank", name="byp_s%d" % b) for b in range(S_BLOCKS)]
-        for c in range(2):
-            for b in range(S_BLOCKS):
-                for e in range(2):
-                    nc.tensor.matmul(
-                        byp_s[b][:],
-                        lhsT=byp0_sb[:, c, e, b * P : (b + 1) * P],
-                        rhs=f0T_sb[:, c, :, e],
-                        start=(c == 0 and e == 0),
-                        stop=(c == 1 and e == 1),
-                    )
+        def to_partitions(rows, n, name):
+            rows_f32 = sb.tile([P, P], F32, name=name + "_f32")
+            nc.vector.tensor_copy(out=rows_f32[:], in_=rows[:])
+            rowsT = bank(7, [P, P], name + "T")
+            nc.tensor.transpose(rowsT[:], rows_f32[:], ident[:])
+            columns = sb.tile([P, n], F32, name=name)
+            nc.vector.tensor_copy(out=columns[:], in_=rowsT[:, 0:n])
+            return columns
+
+        gain = to_partitions(gain_rows, n_w, "gain")
+        gain_s = gain[:, 0:S_BLOCKS]
+        gain_v = gain[:, S_BLOCKS:n_w]
 
         y_v = sb.tile([P, V_BLOCKS, DV, P], F32)
         squares = sb.tile([P, V_BLOCKS, DV, P], F32)
@@ -223,18 +221,31 @@ def tile_feedforward_pb_s_kernel(
             nc.scalar.activation(
                 out=squares[:, b], in_=y_v[:, b], func=ACT.Square, accum_out=sumsq_v[:, b : b + 1]
             )
+        out_sb = sb.tile([P, OUT_S + OUT_V * DV], F32)
+        rstd_v = sb.tile([P, V_BLOCKS], F32)
+        nc.scalar.activation(
+            out=rstd_v[:],
+            in_=sumsq_v[:],
+            func=ACT.Abs_reciprocal_sqrt,
+            scale=1.0 / (P * DV),
+            bias=EPS,
+        )
+        scale_v = sb.tile([P, V_BLOCKS], F32)
+        nc.vector.tensor_tensor(out=scale_v[:], in0=rstd_v[:], in1=gain_v, op=ALU.mult)
+        z_v = sb.tile([P, V_BLOCKS, DV, P], F32)
+        for b in range(V_BLOCKS):
+            nc.scalar.mul(out=z_v[:, b], in_=y_v[:, b], mul=scale_v[:, b : b + 1])
+            zT_v = bank(1 + b, [P, DV, P], "zT_v%d" % b)
+            for d in range(DV):
+                nc.tensor.transpose(zT_v[:, d, :], z_v[:, b, d, :], ident[:])
+            cols = slice(OUT_S + b * P * DV, OUT_S + (b + 1) * P * DV)
+            nc.scalar.copy(
+                out=out_sb[:, cols].rearrange("n (o d) -> n o d", d=DV),
+                in_=zT_v[:].rearrange("n d o -> n o d"),
+            )
+            nc.sync.dma_start(out=out[:, cols], in_=out_sb[:, cols])
 
-        prm_f32 = sb.tile([P, P], F32)
-        nc.vector.tensor_copy(out=prm_f32[:], in_=prm_rows[:])
-        prmT = psum.tile([P, P], F32, tag="bank")
-        nc.tensor.transpose(prmT[:], prm_f32[:], ident[:])
-        prm = sb.tile([P, n_w + S_BLOCKS], F32)
-        nc.vector.tensor_copy(out=prm[:], in_=prmT[:, 0 : n_w + S_BLOCKS])
-        gain_s = prm[:, 0:S_BLOCKS]
-        gain_v = prm[:, S_BLOCKS:n_w]
-        bias_s = prm[:, n_w : n_w + S_BLOCKS]
-
-        lin_s = psum.tile([P, S_BLOCKS, P], F32, tag="bank")
+        lin_s = bank(3, [P, S_BLOCKS, P], "lin_s")
         for b in range(S_BLOCKS):
             for g in range(S_PASSES):
                 nc.tensor.matmul_mx(
@@ -246,85 +257,68 @@ def tile_feedforward_pb_s_kernel(
                     start=(g == 0),
                     stop=(g == S_PASSES - 1),
                 )
-        byp_s_sb = sb.tile([P, S_BLOCKS, P], F32)
-        for b in range(S_BLOCKS):
-            nc.scalar.activation(
-                out=byp_s_sb[:, b, :], in_=byp_s[b][:], func=ACT.Copy, scale=1.0 / math.sqrt(IN_S)
-            )
-
-        out_sb = sb.tile([P, OUT_S + OUT_V * DV], F32)
-        rstd_v = sb.tile([P, V_BLOCKS], F32)
+        lin_s_sb = sb.tile([P, S_BLOCKS, P], F32)
         nc.scalar.activation(
-            out=rstd_v[:],
-            in_=sumsq_v[:],
-            func=ACT.Abs_reciprocal_sqrt,
-            scale=1.0 / (P * DV),
-            bias=EPS,
+            out=lin_s_sb[:], in_=lin_s[:], func=ACT.Copy, scale=1.0 / math.sqrt(HID_S)
         )
+        byp_s = [bank(i, [P, P], "byp_s%d" % b) for b, i in enumerate((0, 4, 5, 6))]
         y_s = sb.tile([P, S_BLOCKS, P], F32)
-        nc.vector.scalar_tensor_tensor(
-            out=y_s[:].rearrange("o b n -> o (b n)"),
-            in0=lin_s[:].rearrange("o b n -> o (b n)"),
-            scalar=1.0 / math.sqrt(HID_S),
-            in1=byp_s_sb[:].rearrange("o b n -> o (b n)"),
-            op0=ALU.mult,
-            op1=ALU.add,
-        )
         stats = sb.tile([P, S_BLOCKS, 6], F32)
         mean_var = sb.tile([P, S_BLOCKS, 2], F32)
         for b in range(S_BLOCKS):
-            nc.vector.bn_stats(out=stats[:, b, :], in_=y_s[:, b, :])
-        scale_v = sb.tile([P, V_BLOCKS], F32)
-        nc.vector.tensor_tensor(out=scale_v[:], in0=rstd_v[:], in1=gain_v, op=ALU.mult)
+            for c in range(2):
+                for e in range(2):
+                    nc.tensor.matmul(
+                        byp_s[b][:],
+                        lhsT=byp0_sb[:, c, e, b * P : (b + 1) * P],
+                        rhs=f0T_sb[:, c, :, e],
+                        start=(c == 0 and e == 0),
+                        stop=(c == 1 and e == 1),
+                    )
         for b in range(S_BLOCKS):
-            nc.vector.bn_aggr(out=mean_var[:, b, :], in_=stats[:, b, :])
-
-        z_v = sb.tile([P, V_BLOCKS, DV, P], F32)
-        zT_v = [psum.tile([P, DV, P], F32, tag="bank", name="zT_v%d" % b) for b in range(V_BLOCKS)]
-
-        def scale_and_transpose_vectors(b):
-            nc.scalar.mul(out=z_v[:, b], in_=y_v[:, b], mul=scale_v[:, b : b + 1])
-            for d in range(DV):
-                nc.tensor.transpose(zT_v[b][:, d, :], z_v[:, b, d, :], ident[:])
-
-        scale_and_transpose_vectors(0)
-        rstd_s = sb.tile([P, S_BLOCKS], F32)
-        nc.scalar.activation(
-            out=rstd_s[:], in_=mean_var[:, :, 1], func=ACT.Abs_reciprocal_sqrt, bias=EPS
-        )
-        scale_and_transpose_vectors(1)
-        centred = sb.tile([P, S_BLOCKS, P], F32)
-        for b in range(S_BLOCKS):
-            nc.vector.tensor_scalar(
-                out=centred[:, b, :],
-                in0=y_s[:, b, :],
-                scalar1=mean_var[:, b, 0:1],
-                scalar2=gain_s[:, b : b + 1],
-                op0=ALU.subtract,
-                op1=ALU.mult,
-            )
-        z_s = sb.tile([P, S_BLOCKS, P], F32)
-        zT_s = [psum.tile([P, 2, P], F32, tag="bank", name="zT_s%d" % half) for half in range(2)]
-        for b in range(S_BLOCKS):
-            nc.vector.tensor_scalar(
-                out=z_s[:, b, :],
-                in0=centred[:, b, :],
-                scalar1=rstd_s[:, b : b + 1],
-                scalar2=bias_s[:, b : b + 1],
+            nc.vector.scalar_tensor_tensor(
+                out=y_s[:, b, :],
+                in0=byp_s[b][:],
+                scalar=1.0 / math.sqrt(IN_S),
+                in1=lin_s_sb[:, b, :],
                 op0=ALU.mult,
                 op1=ALU.add,
             )
-            nc.tensor.transpose(zT_s[b // 2][:, b % 2, :], z_s[:, b, :], ident[:])
-        for b in range(V_BLOCKS):
-            cols = slice(OUT_S + b * P * DV, OUT_S + (b + 1) * P * DV)
-            nc.scalar.copy(
-                out=out_sb[:, cols].rearrange("n (o d) -> n o d", d=DV),
-                in_=zT_v[b][:].rearrange("n d o -> n o d"),
+            nc.vector.bn_stats(out=stats[:, b, :], in_=y_s[:, b, :])
+            nc.vector.bn_aggr(out=mean_var[:, b, :], in_=stats[:, b, :])
+        bias_s = to_partitions(bias_rows, S_BLOCKS, "bias")
+        rstd_s = sb.tile([P, S_BLOCKS], F32)
+        centred = sb.tile([P, S_BLOCKS, P], F32)
+        z_s = sb.tile([P, S_BLOCKS, P], F32)
+        for half in range(2):
+            blocks = (2 * half, 2 * half + 1)
+            nc.scalar.activation(
+                out=rstd_s[:, 2 * half : 2 * half + 2],
+                in_=mean_var[:, 2 * half : 2 * half + 2, 1],
+                func=ACT.Abs_reciprocal_sqrt,
+                bias=EPS,
             )
+            for b in blocks:
+                nc.vector.tensor_scalar(
+                    out=centred[:, b, :],
+                    in0=y_s[:, b, :],
+                    scalar1=mean_var[:, b, 0:1],
+                    scalar2=gain_s[:, b : b + 1],
+                    op0=ALU.subtract,
+                    op1=ALU.mult,
+                )
+            zT_s = bank((0, 3)[half], [P, 2, P], "zT_s%d" % half)
+            for b in blocks:
+                nc.vector.tensor_scalar(
+                    out=z_s[:, b, :],
+                    in0=centred[:, b, :],
+                    scalar1=rstd_s[:, b : b + 1],
+                    scalar2=bias_s[:, b : b + 1],
+                    op0=ALU.mult,
+                    op1=ALU.add,
+                )
+                nc.tensor.transpose(zT_s[:, b % 2, :], z_s[:, b, :], ident[:])
+            cols = slice(2 * half * P, 2 * (half + 1) * P)
+            copy = (nc.scalar.copy, nc.vector.tensor_copy)[half]
+            copy(out=out_sb[:, cols], in_=zT_s[:].rearrange("n b o -> n (b o)"))
             nc.sync.dma_start(out=out[:, cols], in_=out_sb[:, cols])
-        nc.scalar.copy(out=out_sb[:, 0 : 2 * P], in_=zT_s[0][:].rearrange("n b o -> n (b o)"))
-        nc.sync.dma_start(out=out[:, 0 : 2 * P], in_=out_sb[:, 0 : 2 * P])
-        nc.vector.tensor_copy(
-            out=out_sb[:, 2 * P : 4 * P], in_=zT_s[1][:].rearrange("n b o -> n (b o)")
-        )
-        nc.sync.dma_start(out=out[:, 2 * P : 4 * P], in_=out_sb[:, 2 * P : 4 * P])

@@ -90,14 +90,14 @@ def tile_feedforward_pb_s_kernel(
         nc.sync.dma_start(out=w1_words[:].bitcast(I32), in_=lin3_W1_words[0].bitcast(I32))
         f0_sb = sb.tile([P, IN_S], BF16)
         nc.sync.dma_start(out=f0_sb[:], in_=features[:, :IN_S])
+        byp0_sb = sb.tile([P, 2, 2, OUT_S], BF16)
+        nc.sync.dma_start(
+            out=byp0_sb[:], in_=byp_W0.rearrange("(c p e) o -> p c e o", c=2, e=2)
+        )
         w0_words = sb.tile([P, S_PASSES, 2 * OUT_S], U8, align_bytes=64)
         nc.sync.dma_start(
             out=w0_words[:].bitcast(I32), in_=lin3_W0_words.bitcast(I32).rearrange("g p w -> p g w")
         )
-        byp0_sb = sb.tile([P, 2, 2, OUT_S], BF16)
-        byp0_rows = byp_W0.rearrange("(c p e) o -> c p e o", c=2, e=2)
-        for c in range(2):
-            nc.sync.dma_start(out=byp0_sb[:, c], in_=byp0_rows[c])
         load_scale_rows(w0_planes, lin3_W0_scales)
         n_w = S_BLOCKS + V_BLOCKS
         nc.gpsimd.dma_start(out=gain_rows[0:n_w, :], in_=bn_weight.rearrange("(b o) -> b o", o=P))
@@ -245,47 +245,52 @@ def tile_feedforward_pb_s_kernel(
             )
             nc.sync.dma_start(out=out[:, cols], in_=out_sb[:, cols])
 
-        lin_s = bank(3, [P, S_BLOCKS, P], "lin_s")
-        for b in range(S_BLOCKS):
-            for g in range(S_PASSES):
-                nc.tensor.matmul_mx(
-                    out=lin_s[:, b, :],
-                    lhsT=w0_words[:, g, 2 * b * P : 2 * (b + 1) * P].bitcast(FP4X4),
-                    lhsT_scale=w0_planes[:, g, b * P : (b + 1) * P],
-                    rhs=q0_codes[:, g, :].bitcast(FP8X4),
-                    rhs_scale=q0_scales[:, g, :],
-                    start=(g == 0),
-                    stop=(g == S_PASSES - 1),
-                )
-        lin_s_sb = sb.tile([P, S_BLOCKS, P], F32)
-        nc.scalar.activation(
-            out=lin_s_sb[:], in_=lin_s[:], func=ACT.Copy, scale=1.0 / math.sqrt(HID_S)
-        )
-        byp_s = [bank(i, [P, P], "byp_s%d" % b) for b, i in enumerate((0, 4, 5, 6))]
+        byp_s_sb = sb.tile([P, S_BLOCKS, P], F32)
+        for half in range(2):
+            byp_s = bank((0, 4)[half], [P, 2, P], "byp_s%d" % half)
+            for b in (2 * half, 2 * half + 1):
+                for c in range(2):
+                    for e in range(2):
+                        nc.tensor.matmul(
+                            byp_s[:, b % 2, :],
+                            lhsT=byp0_sb[:, c, e, b * P : (b + 1) * P],
+                            rhs=f0T_sb[:, c, :, e],
+                            start=(c == 0 and e == 0),
+                            stop=(c == 1 and e == 1),
+                        )
+            nc.scalar.activation(
+                out=byp_s_sb[:, 2 * half : 2 * half + 2, :],
+                in_=byp_s[:],
+                func=ACT.Copy,
+                scale=1.0 / math.sqrt(IN_S),
+            )
         y_s = sb.tile([P, S_BLOCKS, P], F32)
         stats = sb.tile([P, S_BLOCKS, 6], F32)
         mean_var = sb.tile([P, S_BLOCKS, 2], F32)
-        for b in range(S_BLOCKS):
-            for c in range(2):
-                for e in range(2):
-                    nc.tensor.matmul(
-                        byp_s[b][:],
-                        lhsT=byp0_sb[:, c, e, b * P : (b + 1) * P],
-                        rhs=f0T_sb[:, c, :, e],
-                        start=(c == 0 and e == 0),
-                        stop=(c == 1 and e == 1),
+        for half in range(2):
+            lin_s = bank((3, 5)[half], [P, 2, P], "lin_s%d" % half)
+            for b in (2 * half, 2 * half + 1):
+                for g in range(S_PASSES):
+                    nc.tensor.matmul_mx(
+                        out=lin_s[:, b % 2, :],
+                        lhsT=w0_words[:, g, 2 * b * P : 2 * (b + 1) * P].bitcast(FP4X4),
+                        lhsT_scale=w0_planes[:, g, b * P : (b + 1) * P],
+                        rhs=q0_codes[:, g, :].bitcast(FP8X4),
+                        rhs_scale=q0_scales[:, g, :],
+                        start=(g == 0),
+                        stop=(g == S_PASSES - 1),
                     )
-        for b in range(S_BLOCKS):
             nc.vector.scalar_tensor_tensor(
-                out=y_s[:, b, :],
-                in0=byp_s[b][:],
-                scalar=1.0 / math.sqrt(IN_S),
-                in1=lin_s_sb[:, b, :],
+                out=y_s[:, 2 * half : 2 * half + 2, :].rearrange("o b n -> o (b n)"),
+                in0=lin_s[:].rearrange("o b n -> o (b n)"),
+                scalar=1.0 / math.sqrt(HID_S),
+                in1=byp_s_sb[:, 2 * half : 2 * half + 2, :].rearrange("o b n -> o (b n)"),
                 op0=ALU.mult,
                 op1=ALU.add,
             )
-            nc.vector.bn_stats(out=stats[:, b, :], in_=y_s[:, b, :])
-            nc.vector.bn_aggr(out=mean_var[:, b, :], in_=stats[:, b, :])
+            for b in (2 * half, 2 * half + 1):
+                nc.vector.bn_stats(out=stats[:, b, :], in_=y_s[:, b, :])
+                nc.vector.bn_aggr(out=mean_var[:, b, :], in_=stats[:, b, :])
         bias_s = to_partitions(bias_rows, S_BLOCKS, "bias")
         rstd_s = sb.tile([P, S_BLOCKS], F32)
         centred = sb.tile([P, S_BLOCKS, P], F32)
@@ -307,7 +312,7 @@ def tile_feedforward_pb_s_kernel(
                     op0=ALU.subtract,
                     op1=ALU.mult,
                 )
-            zT_s = bank((0, 3)[half], [P, 2, P], "zT_s%d" % half)
+            zT_s = bank((0, 4)[half], [P, 2, P], "zT_s%d" % half)
             for b in blocks:
                 nc.vector.tensor_scalar(
                     out=z_s[:, b, :],

@@ -122,7 +122,7 @@ def tile_feedforward_pb_s_kernel(
         grouped1 = sb.tile([P, DV, P, 4], BF16, align_bytes=64)
         q1_codes = sb.tile([P, DV, P], U32, align_bytes=64)
         q1_scales = sb.tile([P, DV, P], U8, align_bytes=64)
-        for d, copy in ((0, nc.vector.tensor_copy), (1, nc.scalar.copy), (2, nc.scalar.copy)):
+        for d, copy in ((0, nc.scalar.copy), (1, nc.scalar.copy), (2, nc.scalar.copy)):
             h1_pairs = h1_sorted[:, d].rearrange("n u p e -> n (u p e)").bitcast(F32)
             h1T = bank(1 + d, [P, 2, P], "h1T%d" % d)
             for u in range(2):

@@ -23,7 +23,7 @@ S_BLOCKS = OUT_S // P
 V_BLOCKS = OUT_V // P
 S_PASSES = HID_S // 512
 EPS = 1e-5
-WARM_UP_MATMULS = 3
+WARM_UP_MATMULS = 6
 
 FLOPS = 2 * P * (HID_S * OUT_S + DV * HID_V * OUT_V + IN_S * OUT_S + DV * IN_V * OUT_V)
 

@@ -58,7 +58,7 @@ def tile_feedforward_pb_s_kernel(
                 )
 
         w1_planes = sb.tile([P, 1, OUT_V], U8, align_bytes=64)
-        nc.vector.memset(w1_planes[:].bitcast(I32), 0)
+        nc.gpsimd.memset(w1_planes[:].bitcast(F32), 0.0)
         zeros = sb.tile([P, P], F32)
         nc.vector.memset(zeros[:], 0.0)
         idle_ps = bank(0, [P, P], "idle_ps")
@@ -76,12 +76,11 @@ def tile_feedforward_pb_s_kernel(
         bias_rows = sb.tile([P, P], BF16)
         nc.vector.memset(bias_rows[:], 0.0)
 
-        f1_sb = sb.tile([P, IN_V * DV], BF16)
-        nc.scalar.dma_start(out=f1_sb[:], in_=features[:, IN_S:])
-        nc.scalar.activation(out=warm[:], in_=warm[:], func=ACT.Abs_reciprocal_sqrt)
         load_scale_rows(w1_planes, lin3_W1_scales)
         h1_sb = sb.tile([P, HID_V * DV], BF16)
         nc.sync.dma_start(out=h1_sb[:], in_=h2[:, HID_S:])
+        f1_sb = sb.tile([P, IN_V * DV], BF16)
+        nc.sync.dma_start(out=f1_sb[:], in_=features[:, IN_S:])
         byp1_sb = sb.tile([P, 2, OUT_V], BF16)
         nc.sync.dma_start(out=byp1_sb[:], in_=byp_W1.rearrange("(q a) o -> q a o", a=2))
         h0_sb = sb.tile([P, HID_S], BF16)
@@ -99,9 +98,16 @@ def tile_feedforward_pb_s_kernel(
             out=w0_words[:].bitcast(I32), in_=lin3_W0_words.bitcast(I32).rearrange("g p w -> p g w")
         )
         load_scale_rows(w0_planes, lin3_W0_scales)
+        nc.scalar.activation(out=warm[:], in_=warm[:], func=ACT.Abs_reciprocal_sqrt)
         n_w = S_BLOCKS + V_BLOCKS
         nc.gpsimd.dma_start(out=gain_rows[0:n_w, :], in_=bn_weight.rearrange("(b o) -> b o", o=P))
         nc.gpsimd.dma_start(out=bias_rows[0:S_BLOCKS, :], in_=bn_bias.rearrange("(b o) -> b o", o=P))
+
+        h1_sorted = sb.tile([P, DV, 2, P, 2], BF16)
+        h1_by_d = h1_sb[:].rearrange("n (p u e d) -> n d u p e", u=2, e=2, d=DV)
+        nc.vector.tensor_copy(out=h1_sorted[:, 0], in_=h1_by_d[:, 0])
+        nc.scalar.copy(out=h1_sorted[:, 2], in_=h1_by_d[:, 2])
+        nc.vector.tensor_copy(out=h1_sorted[:, 1], in_=h1_by_d[:, 1])
 
         f1_pairs = f1_sb[:].bitcast(F32)
         f1T = bank(4, [P, DV, P], "f1T")
@@ -112,12 +118,6 @@ def tile_feedforward_pb_s_kernel(
             out=f1T_sb[:].rearrange("p j n e -> p (j n e)").bitcast(F32),
             in_=f1T[:].rearrange("p j n -> p (j n)"),
         )
-
-        h1_sorted = sb.tile([P, DV, 2, P, 2], BF16)
-        h1_by_d = h1_sb[:].rearrange("n (p u e d) -> n d u p e", u=2, e=2, d=DV)
-        nc.vector.tensor_copy(out=h1_sorted[:, 0], in_=h1_by_d[:, 0])
-        nc.scalar.copy(out=h1_sorted[:, 2], in_=h1_by_d[:, 2])
-        nc.vector.tensor_copy(out=h1_sorted[:, 1], in_=h1_by_d[:, 1])
 
         grouped1 = sb.tile([P, DV, P, 4], BF16, align_bytes=64)
         q1_codes = sb.tile([P, DV, P], U32, align_bytes=64)

import math
from contextlib import ExitStack

import concourse.mybir as mybir
from concourse.masks import make_identity

BF16 = mybir.dt.bfloat16
F32 = mybir.dt.float32
I32 = mybir.dt.int32
U32 = mybir.dt.uint32
U8 = mybir.dt.uint8
FP8X4 = mybir.dt.float8_e4m3fn_x4
FP4X4 = mybir.dt.float4_e2m1fn_x4
ALU = mybir.AluOpType
ACT = mybir.ActivationFunctionType

P = 128
DV = 3
HID_S, HID_V = 1024, 512
IN_S, IN_V = 512, 256
OUT_S, OUT_V = 512, 256
S_BLOCKS = OUT_S // P
V_BLOCKS = OUT_V // P
S_PASSES = HID_S // 512
EPS = 1e-5
WARM_UP_MATMULS = 6

FLOPS = 2 * P * (HID_S * OUT_S + DV * HID_V * OUT_V + IN_S * OUT_S + DV * IN_V * OUT_V)


def tile_feedforward_pb_s_kernel(
    tc,
    h2,
    features,
    lin3_W0_words,
    lin3_W0_scales,
    lin3_W1_words,
    lin3_W1_scales,
    byp_W0,
    byp_W1,
    bn_weight,
    bn_bias,
    out,
):
    nc = tc.nc
    with ExitStack() as ctx:
        sb = ctx.enter_context(tc.tile_pool(name="sb", bufs=1))
        psum = ctx.enter_context(tc.psum_pool(name="psum", bufs=1))

        def bank(i, shape, name):
            return psum.tile(shape, F32, tag="bank%d" % i, name=name)

        def load_scale_rows(planes, rows):
            for quad in range(4):
                nc.sync.dma_start(
                    out=planes[32 * quad : 32 * quad + 4].bitcast(I32),
                    in_=rows.bitcast(I32)[:, 4 * quad : 4 * quad + 4, :].rearrange("g r w -> r g w"),
                )

        w1_planes = sb.tile([P, 1, OUT_V], U8, align_bytes=64)
        nc.gpsimd.memset(w1_planes[:].bitcast(F32), 0.0)
        zeros = sb.tile([P, P], F32)
        nc.vector.memset(zeros[:], 0.0)
        idle_ps = bank(0, [P, P], "idle_ps")
        for i in range(WARM_UP_MATMULS):
            nc.tensor.matmul(idle_ps[:], lhsT=zeros[:], rhs=zeros[:], start=True, stop=True)
        w0_planes = sb.tile([P, S_PASSES, OUT_S], U8, align_bytes=64)
        ident = sb.tile([P, P], F32)
        nc.vector.memset(ident[:], 0.0)
        make_identity(nc, ident[:], nomemset=True)
        warm = sb.tile([P, 1], F32)
        nc.vector.memset(warm[:], 1.0)
        nc.vector.memset(w0_planes[:].bitcast(I32), 0)
        gain_rows = sb.tile([P, P], BF16)
        nc.vector.memset(gain_rows[:], 0.0)
        bias_rows = sb.tile([P, P], BF16)
        nc.vector.memset(bias_rows[:], 0.0)

        load_scale_rows(w1_planes, lin3_W1_scales)
        h1_sb = sb.tile([P, HID_V * DV], BF16)
        nc.sync.dma_start(out=h1_sb[:], in_=h2[:, HID_S:])
        f1_sb = sb.tile([P, IN_V * DV], BF16)
        nc.sync.dma_start(out=f1_sb[:], in_=features[:, IN_S:])
        byp1_sb = sb.tile([P, 2, OUT_V], BF16)
        nc.sync.dma_start(out=byp1_sb[:], in_=byp_W1.rearrange("(q a) o -> q a o", a=2))
        h0_sb = sb.tile([P, HID_S], BF16)
        nc.sync.dma_start(out=h0_sb[:], in_=h2[:, :HID_S])
        w1_words = sb.tile([P, 2 * OUT_V], U8, align_bytes=64)
        nc.sync.dma_start(out=w1_words[:].bitcast(I32), in_=lin3_W1_words[0].bitcast(I32))
        f0_sb = sb.tile([P, IN_S], BF16)
        nc.sync.dma_start(out=f0_sb[:], in_=features[:, :IN_S])
        byp0_sb = sb.tile([P, 2, 2, OUT_S], BF16)
        nc.sync.dma_start(
            out=byp0_sb[:], in_=byp_W0.rearrange("(c p e) o -> p c e o", c=2, e=2)
        )
        w0_words = sb.tile([P, S_PASSES, 2 * OUT_S], U8, align_bytes=64)
        nc.sync.dma_start(
            out=w0_words[:].bitcast(I32), in_=lin3_W0_words.bitcast(I32).rearrange("g p w -> p g w")
        )
        load_scale_rows(w0_planes, lin3_W0_scales)
        nc.scalar.activation(out=warm[:], in_=warm[:], func=ACT.Abs_reciprocal_sqrt)
        n_w = S_BLOCKS + V_BLOCKS
        nc.gpsimd.dma_start(out=gain_rows[0:n_w, :], in_=bn_weight.rearrange("(b o) -> b o", o=P))
        nc.gpsimd.dma_start(out=bias_rows[0:S_BLOCKS, :], in_=bn_bias.rearrange("(b o) -> b o", o=P))

        h1_sorted = sb.tile([P, DV, 2, P, 2], BF16)
        h1_by_d = h1_sb[:].rearrange("n (p u e d) -> n d u p e", u=2, e=2, d=DV)
        nc.vector.tensor_copy(out=h1_sorted[:, 0], in_=h1_by_d[:, 0])
        nc.scalar.copy(out=h1_sorted[:, 2], in_=h1_by_d[:, 2])
        nc.vector.tensor_copy(out=h1_sorted[:, 1], in_=h1_by_d[:, 1])

        f1_pairs = f1_sb[:].bitcast(F32)
        f1T = bank(4, [P, DV, P], "f1T")
        for j in range(DV):
            nc.tensor.transpose(f1T[:, j, :], f1_pairs[:, j::DV], ident[:])
        f1T_sb = sb.tile([P, DV, P, 2], BF16)
        nc.scalar.copy(
            out=f1T_sb[:].rearrange("p j n e -> p (j n e)").bitcast(F32),
            in_=f1T[:].rearrange("p j n -> p (j n)"),
        )

        grouped1 = sb.tile([P, DV, P, 4], BF16, align_bytes=64)
        q1_codes = sb.tile([P, DV, P], U32, align_bytes=64)
        q1_scales = sb.tile([P, DV, P], U8, align_bytes=64)
        for d, copy in ((0, nc.scalar.copy), (1, nc.scalar.copy), (2, nc.scalar.copy)):
            h1_pairs = h1_sorted[:, d].rearrange("n u p e -> n (u p e)").bitcast(F32)
            h1T = bank(1 + d, [P, 2, P], "h1T%d" % d)
            for u in range(2):
                nc.tensor.transpose(h1T[:, u, :], h1_pairs[:, u * P : (u + 1) * P], ident[:])
            copy(out=grouped1[:, d].bitcast(F32), in_=h1T[:].rearrange("p u n -> p n u"))
        for d in range(DV):
            nc.vector.quantize_mx(
                out=q1_codes[:, d].bitcast(FP8X4),
                scales=q1_scales[:, d],
                in_=grouped1[:, d].rearrange("p n t -> p (n t)"),
            )

        byp_v = [bank(5 + b, [P, DV, P], "byp_v%d" % b) for b in range(V_BLOCKS)]
        for b in range(V_BLOCKS):
            for d in range(DV):
                for a in range(2):
                    j, e = divmod(DV * a + d, 2)
                    nc.tensor.matmul(
                        byp_v[b][:, d, :],
                        lhsT=byp1_sb[:, a, b * P : (b + 1) * P],
                        rhs=f1T_sb[:, j, :, e],
                        start=(a == 0),
                        stop=(a == 1),
                    )

        h0_pairs = h0_sb[:].bitcast(F32)
        h0T = bank(0, [P, S_PASSES, 2, P], "h0T")
        for g in range(S_PASSES):
            for u in range(2):
                nc.tensor.transpose(
                    h0T[:, g, u, :], h0_pairs[:, 256 * g + u : 256 * (g + 1) : 2], ident[:]
                )
        grouped0 = sb.tile([P, S_PASSES, P, 4], BF16, align_bytes=64)
        nc.scalar.copy(out=grouped0[:].bitcast(F32), in_=h0T[:].rearrange("p g u n -> p g n u"))
        q0_codes = sb.tile([P, S_PASSES, P], U32, align_bytes=64)
        q0_scales = sb.tile([P, S_PASSES, P], U8, align_bytes=64)
        nc.vector.quantize_mx(
            out=q0_codes[:].rearrange("p g n -> p (g n)").bitcast(FP8X4),
            scales=q0_scales[:].rearrange("p g n -> p (g n)"),
            in_=grouped0[:].rearrange("p g n t -> p (g n t)"),
        )

        f0_pairs = f0_sb[:].bitcast(F32)
        f0T = bank(7, [P, 2, P], "f0T")
        for c in range(2):
            nc.tensor.transpose(f0T[:, c, :], f0_pairs[:, c * P : (c + 1) * P], ident[:])
        f0T_sb = sb.tile([P, 2, P, 2], BF16)
        nc.vector.tensor_copy(
            out=f0T_sb[:].rearrange("p c n e -> p (c n e)").bitcast(F32),
            in_=f0T[:].rearrange("p c n -> p (c n)"),
        )

        byp_v_sb = sb.tile([P, V_BLOCKS, DV, P], F32)
        for b in range(V_BLOCKS):
            nc.scalar.activation(
                out=byp_v_sb[:, b], in_=byp_v[b][:], func=ACT.Copy, scale=1.0 / math.sqrt(IN_V)
            )
        lin_v = [bank(1 + b, [P, DV, P], "lin_v%d" % b) for b in range(V_BLOCKS)]
        for b in range(V_BLOCKS):
            for d in range(DV):
                nc.tensor.matmul_mx(
                    out=lin_v[b][:, d, :],
                    lhsT=w1_words[:, 2 * b * P : 2 * (b + 1) * P].bitcast(FP4X4),
                    lhsT_scale=w1_planes[:, 0, b * P : (b + 1) * P],
                    rhs=q1_codes[:, d, :].bitcast(FP8X4),
                    rhs_scale=q1_scales[:, d, :],
                    start=True,
                    stop=True,
                )

        def to_partitions(rows, n, name):
            rows_f32 = sb.tile([P, P], F32, name=name + "_f32")
            nc.vector.tensor_copy(out=rows_f32[:], in_=rows[:])
            rowsT = bank(7, [P, P], name + "T")
            nc.tensor.transpose(rowsT[:], rows_f32[:], ident[:])
            columns = sb.tile([P, n], F32, name=name)
            nc.vector.tensor_copy(out=columns[:], in_=rowsT[:, 0:n])
            return columns

        gain = to_partitions(gain_rows, n_w, "gain")
        gain_s = gain[:, 0:S_BLOCKS]
        gain_v = gain[:, S_BLOCKS:n_w]

        y_v = sb.tile([P, V_BLOCKS, DV, P], F32)
        squares = sb.tile([P, V_BLOCKS, DV, P], F32)
        sumsq_v = sb.tile([P, V_BLOCKS], F32)
        for b in range(V_BLOCKS):
            nc.vector.scalar_tensor_tensor(
                out=y_v[:, b].rearrange("o d n -> o (d n)"),
                in0=lin_v[b][:].rearrange("o d n -> o (d n)"),
                scalar=1.0 / math.sqrt(HID_V),
                in1=byp_v_sb[:, b].rearrange("o d n -> o (d n)"),
                op0=ALU.mult,
                op1=ALU.add,
            )
            nc.scalar.activation(
                out=squares[:, b], in_=y_v[:, b], func=ACT.Square, accum_out=sumsq_v[:, b : b + 1]
            )
        out_sb = sb.tile([P, OUT_S + OUT_V * DV], F32)
        rstd_v = sb.tile([P, V_BLOCKS], F32)
        nc.scalar.activation(
            out=rstd_v[:],
            in_=sumsq_v[:],
            func=ACT.Abs_reciprocal_sqrt,
            scale=1.0 / (P * DV),
            bias=EPS,
        )
        scale_v = sb.tile([P, V_BLOCKS], F32)
        nc.vector.tensor_tensor(out=scale_v[:], in0=rstd_v[:], in1=gain_v, op=ALU.mult)
        z_v = sb.tile([P, V_BLOCKS, DV, P], F32)
        for b in range(V_BLOCKS):
            nc.scalar.mul(out=z_v[:, b], in_=y_v[:, b], mul=scale_v[:, b : b + 1])
            zT_v = bank(1 + b, [P, DV, P], "zT_v%d" % b)
            for d in range(DV):
                nc.tensor.transpose(zT_v[:, d, :], z_v[:, b, d, :], ident[:])
            cols = slice(OUT_S + b * P * DV, OUT_S + (b + 1) * P * DV)
            nc.scalar.copy(
                out=out_sb[:, cols].rearrange("n (o d) -> n o d", d=DV),
                in_=zT_v[:].rearrange("n d o -> n o d"),
            )
            nc.sync.dma_start(out=out[:, cols], in_=out_sb[:, cols])

        byp_s_sb = sb.tile([P, S_BLOCKS, P], F32)
        for half in range(2):
            byp_s = bank((0, 4)[half], [P, 2, P], "byp_s%d" % half)
            for b in (2 * half, 2 * half + 1):
                for c in range(2):
                    for e in range(2):
                        nc.tensor.matmul(
                            byp_s[:, b % 2, :],
                            lhsT=byp0_sb[:, c, e, b * P : (b + 1) * P],
                            rhs=f0T_sb[:, c, :, e],
                            start=(c == 0 and e == 0),
                            stop=(c == 1 and e == 1),
                        )
            nc.scalar.activation(
                out=byp_s_sb[:, 2 * half : 2 * half + 2, :],
                in_=byp_s[:],
                func=ACT.Copy,
                scale=1.0 / math.sqrt(IN_S),
            )
        y_s = sb.tile([P, S_BLOCKS, P], F32)
        stats = sb.tile([P, S_BLOCKS, 6], F32)
        mean_var = sb.tile([P, S_BLOCKS, 2], F32)
        for half in range(2):
            lin_s = bank((3, 5)[half], [P, 2, P], "lin_s%d" % half)
            for b in (2 * half, 2 * half + 1):
                for g in range(S_PASSES):
                    nc.tensor.matmul_mx(
                        out=lin_s[:, b % 2, :],
                        lhsT=w0_words[:, g, 2 * b * P : 2 * (b + 1) * P].bitcast(FP4X4),
                        lhsT_scale=w0_planes[:, g, b * P : (b + 1) * P],
                        rhs=q0_codes[:, g, :].bitcast(FP8X4),
                        rhs_scale=q0_scales[:, g, :],
                        start=(g == 0),
                        stop=(g == S_PASSES - 1),
                    )
            nc.vector.scalar_tensor_tensor(
                out=y_s[:, 2 * half : 2 * half + 2, :].rearrange("o b n -> o (b n)"),
                in0=lin_s[:].rearrange("o b n -> o (b n)"),
                scalar=1.0 / math.sqrt(HID_S),
                in1=byp_s_sb[:, 2 * half : 2 * half + 2, :].rearrange("o b n -> o (b n)"),
                op0=ALU.mult,
                op1=ALU.add,
            )
            for b in (2 * half, 2 * half + 1):
                nc.vector.bn_stats(out=stats[:, b, :], in_=y_s[:, b, :])
                nc.vector.bn_aggr(out=mean_var[:, b, :], in_=stats[:, b, :])
        bias_s = to_partitions(bias_rows, S_BLOCKS, "bias")
        rstd_s = sb.tile([P, S_BLOCKS], F32)
        centred = sb.tile([P, S_BLOCKS, P], F32)
        z_s = sb.tile([P, S_BLOCKS, P], F32)
        for half in range(2):
            blocks = (2 * half, 2 * half + 1)
            nc.scalar.activation(
                out=rstd_s[:, 2 * half : 2 * half + 2],
                in_=mean_var[:, 2 * half : 2 * half + 2, 1],
                func=ACT.Abs_reciprocal_sqrt,
                bias=EPS,
            )
            for b in blocks:
                nc.vector.tensor_scalar(
                    out=centred[:, b, :],
                    in0=y_s[:, b, :],
                    scalar1=mean_var[:, b, 0:1],
                    scalar2=gain_s[:, b : b + 1],
                    op0=ALU.subtract,
                    op1=ALU.mult,
                )
            zT_s = bank((0, 4)[half], [P, 2, P], "zT_s%d" % half)
            for b in blocks:
                nc.vector.tensor_scalar(
                    out=z_s[:, b, :],
                    in0=centred[:, b, :],
                    scalar1=rstd_s[:, b : b + 1],
                    scalar2=bias_s[:, b : b + 1],
                    op0=ALU.mult,
                    op1=ALU.add,
                )
                nc.tensor.transpose(zT_s[:, b % 2, :], z_s[:, b, :], ident[:])
            cols = slice(2 * half * P, 2 * (half + 1) * P)
            copy = (nc.scalar.copy, nc.vector.tensor_copy)[half]
            copy(out=out_sb[:, cols], in_=zT_s[:].rearrange("n b o -> n (b o)"))
            nc.sync.dma_start(out=out[:, cols], in_=out_sb[:, cols])
